import numpy as np
import ml_dtypes


def mxq(x, axis, fmt="e4m3"):
    dtype, down = {"e4m3": (ml_dtypes.float8_e4m3fn, 7), "e5m2": (ml_dtypes.float8_e5m2, 14)}[fmt]
    v = np.moveaxis(np.asarray(x, np.float32).astype(ml_dtypes.bfloat16).astype(np.float64), axis, -1)
    blocks = v.reshape(v.shape[:-1] + (-1, 32))
    amax = np.abs(blocks).max(-1, keepdims=True)
    byte = np.maximum(np.where(amax > 0, np.frexp(amax)[1] - 1 + 127, 0) - down, 1)
    scale = np.exp2(byte - 127.0)
    codes = (blocks / scale).astype(np.float32).astype(dtype).astype(np.float64)
    return np.moveaxis((codes * scale).reshape(v.shape), -1, axis)


WIDE = False


def mx_kscale(k):
    if not WIDE:
        return np.ones(k)
    levels = np.array([10, -10, 5, -5, 0])
    a = np.random.permutation(np.resize(levels, k // 512 * 4)).reshape(k // 512, 4)
    idx = np.arange(k)
    return np.exp2(a[idx // 512, idx % 128 // 32])


BF16 = ml_dtypes.bfloat16


def bf(x):
    return np.asarray(x, np.float32).astype(BF16)


def f64(x):
    return np.asarray(x).astype(np.float64)


E2M1 = np.array([0.0, 0.5, 1.0, 1.5, 2.0, 3.0, 4.0, 6.0, -0.0, -0.5, -1.0, -1.5, -2.0, -3.0, -4.0, -6.0])


def pack_weight(w, fmt):
    k, n = w.shape
    w = f64(bf(w)).reshape(k // 32, 32, n)
    amax = np.abs(w).max(1)
    if fmt == "e4m3":
        byte = np.frexp(amax)[1] - 1 + 127 - 7
    else:
        mant, ex = np.frexp(amax / 6.0)
        byte = np.where(mant > 0.5, ex, ex - 1) + 127
    byte = np.clip(np.where(amax > 0, byte, 1), 1, 254)
    scaled = (w * np.exp2(127.0 - byte)[:, None, :]).reshape(k, n).astype(np.float32)
    by_word = np.ascontiguousarray(scaled.reshape(k // 512, 128, 4, n).transpose(0, 1, 3, 2))
    if fmt == "e4m3":
        words = by_word.astype(ml_dtypes.float8_e4m3fn).view(np.uint8)
    else:
        c = by_word.astype(ml_dtypes.float4_e2m1fn).view(np.uint8) & 0xF
        words = c[..., 0::2] | (c[..., 1::2] << 4)
    return np.ascontiguousarray(words), np.ascontiguousarray(byte.astype(np.uint8).reshape(k // 512, 16, n))


def unpack_weight(words, scales, fmt):
    g, p, n, _ = words.shape
    if fmt == "e4m3":
        vals = np.ascontiguousarray(words).view(ml_dtypes.float8_e4m3fn).astype(np.float64)
    else:
        nib = np.empty((g, p, n, 4), np.uint8)
        nib[..., 0::2] = words & 0xF
        nib[..., 1::2] = words >> 4
        vals = E2M1[nib]
    vals = vals * np.repeat(np.exp2(scales.astype(np.float64) - 127.0), 8, axis=1)[..., None]
    return vals.transpose(0, 1, 3, 2).reshape(g * 512, n)

def pack4(w):
    words, scales = pack_weight(w, "e2m1")
    return words.reshape(words.shape[0], 128, -1), scales


def unpack4(words, scales):
    return unpack_weight(words.reshape(words.shape[0], 128, -1, 2), scales, "e2m1")


B, N, NODE_IN, EDGE_IN, EDGE_OUT = 2, 32, 384, 256, 1024
D_IN = 2 * NODE_IN + EDGE_IN
HID = 2 * EDGE_OUT
NEG_SLOPE = 0.1


def leaky_relu(v):
    return np.where(v >= 0.0, v, NEG_SLOPE * v)


def setup_inputs():
    s = mx_kscale(D_IN)
    sn, se = s[:NODE_IN], s[2 * NODE_IN:]
    st = np.concatenate([sn, sn, se])
    node_fts = bf(np.random.standard_normal((B, N, NODE_IN)) * sn)
    edge_fts = bf(np.random.standard_normal((B, N * N, EDGE_IN)) * se)
    wt = np.random.standard_normal((HID, D_IN)) / np.sqrt(D_IN) / st
    words, scales = pack4(np.ascontiguousarray(wt.T))
    return {"node_fts": node_fts,
            "edge_fts": edge_fts,
            "Wt_words": words,
            "Wt_scales": scales}


def reference(node_fts, edge_fts, Wt_words, Wt_scales):
    node = f64(node_fts)
    src = np.repeat(node, N, axis=1)
    dst = np.tile(node, (1, N, 1))
    triplet = np.concatenate([src, dst, f64(edge_fts)], axis=-1)
    return leaky_relu(mxq(triplet, 2, "e4m3") @ unpack4(Wt_words, Wt_scales))

@@ -1,0 +1,196 @@
+from contextlib import ExitStack
+
+import concourse.mybir as mybir
+from concourse.masks import make_identity
+
+F32 = mybir.dt.float32
+BF16 = mybir.dt.bfloat16
+I32 = mybir.dt.int32
+U32 = mybir.dt.uint32
+U8 = mybir.dt.uint8
+FP8X4 = mybir.dt.float8_e4m3fn_x4
+FP4X4 = mybir.dt.float4_e2m1fn_x4
+COPY = mybir.ActivationFunctionType.Copy
+MAX = mybir.AluOpType.max
+
+P = 128
+GRAPHS = 2
+NODES = 32
+NODE_IN = 384
+EDGE_IN = 256
+HID = 2048
+NEG_SLOPE = 0.1
+ROWS = GRAPHS * NODES * NODES
+ROW_TILES = ROWS // P
+TILES_PER_GRAPH = ROW_TILES // GRAPHS
+I_PER_TILE = P // NODES
+BANK = 512
+COL_TILES = HID // BANK
+PASSES = 2
+SRC_PARTS = NODE_IN // 4
+EDGE_PARTS = EDGE_IN // 4
+ALL_NODES = GRAPHS * NODES
+REP = 4
+
+FLOPS = 2 * ROWS * (2 * NODE_IN + EDGE_IN) * HID
+
+
+def tile_edge_update_only_pa_kernel(tc, node_fts, edge_fts, Wt_words, Wt_scales, out):
+    nc = tc.nc
+    with ExitStack() as ctx:
+        keep = ctx.enter_context(tc.tile_pool(name="keep", bufs=1))
+        tenths = ctx.enter_context(tc.tile_pool(name="tenths", bufs=4))
+        results = ctx.enter_context(tc.tile_pool(name="results", bufs=3))
+        psum = ctx.enter_context(tc.psum_pool(name="psum", bufs=8))
+
+        ident = keep.tile([P, P], F32)
+        nodes2 = keep.tile([P, 2, NODE_IN], BF16)
+        edge_sb = keep.tile([P, ROW_TILES + 1, EDGE_IN], BF16)
+        w_words = keep.tile([P, PASSES, 2 * HID], U8, align_bytes=64)
+        w_scales = keep.tile([P, PASSES, HID], U8, align_bytes=64)
+        node_grouped = keep.tile([P, 2 * ALL_NODES * REP, 4], BF16, align_bytes=64)
+        node_codes = keep.tile([P, 2 * ALL_NODES * REP], U32, align_bytes=64)
+        node_scales = keep.tile([P, 2 * ALL_NODES * REP], U8, align_bytes=64)
+        codes0 = keep.tile([P, ROW_TILES, P], U32, align_bytes=64)
+        scales0 = keep.tile([P, ROW_TILES, P], U8, align_bytes=64)
+        codes1 = keep.tile([P, ROW_TILES, P], U32, align_bytes=64)
+        scales1 = keep.tile([P, ROW_TILES, P], U8, align_bytes=64)
+        edge_grouped = [
+            [keep.tile([P, P, 4], BF16, name="edge_grouped_%d_%d" % (b, s), align_bytes=64) for s in range(2)]
+            for b in range(GRAPHS)
+        ]
+
+        nc.vector.memset(w_scales[:].rearrange("p g n -> p (g n)").bitcast(I32), 0)
+        nc.vector.memset(node_scales[:].bitcast(I32), 0)
+        nc.gpsimd.memset(nodes2[ALL_NODES:P], 0.0)
+        nc.gpsimd.memset(edge_sb[:, 0, :], 0.0)
+        make_identity(nc, ident[:])
+
+        node_rows = node_fts.flatten_outer_dims()
+        nc.scalar.dma_start(
+            out=nodes2[0:ALL_NODES],
+            in_=node_rows.unsqueeze(1).to_broadcast([ALL_NODES, 2, NODE_IN]),
+        )
+        edge_rows = edge_fts.flatten_outer_dims().rearrange("(j r) e -> r j e", r=P)
+        for q in range(4):
+            nc.sync.dma_start(out=edge_sb[:, 1 + 4 * q : 5 + 4 * q, :], in_=edge_rows[:, 4 * q : 4 * q + 4, :])
+        for q in range(4):
+            nc.sync.dma_start(
+                out=w_scales[32 * q : 32 * q + 4].bitcast(I32),
+                in_=Wt_scales[:, 4 * q : 4 * q + 4, :].rearrange("g r n -> r g n").bitcast(I32),
+            )
+        for g in range(PASSES):
+            nc.sync.dma_start(out=w_words[:, g, :].bitcast(I32), in_=Wt_words[g].bitcast(I32))
+
+        node_words = nodes2[:].rearrange("p c f -> p (c f)").bitcast(F32)
+        first_t = psum.tile([P, BANK], F32, tag="bank")
+        second_t = psum.tile([P, BANK], F32, tag="bank")
+        first_planes = first_t[:, 0 : 2 * P].rearrange("p (u n) -> p u n", u=2)
+        second_planes = second_t[:, 0 : 2 * P].rearrange("p (u n) -> p u n", u=2)
+        for u in range(2):
+            nc.tensor.transpose(first_planes[:, u, :], node_words[:, u : 2 * P : 2], ident[:])
+        for u in range(2):
+            nc.tensor.transpose(second_planes[:, u, :], node_words[:, 64 + u : 64 + 2 * P : 2], ident[:])
+
+        grouped_words = node_grouped[:].rearrange("p c t -> p (c t)").bitcast(F32)
+        half = 2 * ALL_NODES * REP
+        nc.vector.tensor_copy(
+            out=grouped_words[:, 0:half].rearrange("p (n r u) -> p n r u", r=REP, u=2),
+            in_=first_planes[:, :, 0:ALL_NODES]
+            .rearrange("p u n -> p n u")
+            .unsqueeze(2)
+            .to_broadcast([P, ALL_NODES, REP, 2]),
+        )
+        for b in range(GRAPHS):
+            nc.vector.tensor_copy(
+                out=grouped_words[:, half + 2 * P * b : half + 2 * P * (b + 1)].rearrange(
+                    "p (i k u) -> p i k u", i=I_PER_TILE, u=2
+                ),
+                in_=first_planes[:, :, NODES * b : NODES * (b + 1)]
+                .rearrange("p u k -> p k u")
+                .unsqueeze(1)
+                .to_broadcast([P, I_PER_TILE, NODES, 2]),
+            )
+            for s in range(2):
+                nc.scalar.copy(
+                    out=edge_grouped[b][s][0:EDGE_PARTS]
+                    .rearrange("p r t -> p (r t)")
+                    .bitcast(F32)
+                    .rearrange("p (i k u) -> p i k u", i=I_PER_TILE, u=2),
+                    in_=second_planes[0:EDGE_PARTS, :, NODES * b : NODES * (b + 1)]
+                    .rearrange("p u k -> p k u")
+                    .unsqueeze(1)
+                    .to_broadcast([EDGE_PARTS, I_PER_TILE, NODES, 2]),
+                )
+        nc.vector.quantize_mx(
+            out=node_codes[:].bitcast(FP8X4),
+            scales=node_scales[:],
+            in_=node_grouped[:].rearrange("p c t -> p (c t)"),
+        )
+
+        node_codes_i = node_codes[:].bitcast(I32)
+        node_scales_i = node_scales[:].bitcast(I32)
+        codes0_i = codes0[:].bitcast(I32)
+        scales0_i = scales0[:].rearrange("p j c -> p (j c)").bitcast(I32)
+        n_src = ALL_NODES * REP
+        nc.vector.tensor_copy(
+            out=codes0_i[0:SRC_PARTS].rearrange("p j (i k) -> p (j i) k", k=NODES),
+            in_=node_codes_i[0:SRC_PARTS, 0:n_src:REP].unsqueeze(2).to_broadcast([SRC_PARTS, ALL_NODES, NODES]),
+        )
+        nc.vector.tensor_copy(
+            out=scales0_i[0:SRC_PARTS].rearrange("p (n w) -> p n w", w=NODES // 4),
+            in_=node_scales_i[0:SRC_PARTS, 0:ALL_NODES].unsqueeze(2).to_broadcast([SRC_PARTS, ALL_NODES, NODES // 4]),
+        )
+        nc.vector.tensor_copy(
+            out=codes0_i[SRC_PARTS:P].rearrange("p (b g) c -> p b g c", b=GRAPHS),
+            in_=node_codes_i[SRC_PARTS:P, n_src : 2 * n_src]
+            .rearrange("p (b c) -> p b c", b=GRAPHS)
+            .unsqueeze(2)
+            .to_broadcast([P - SRC_PARTS, GRAPHS, TILES_PER_GRAPH, P]),
+        )
+        nc.vector.tensor_copy(
+            out=scales0_i[SRC_PARTS:P].rearrange("p (b g w) -> p b g w", b=GRAPHS, g=TILES_PER_GRAPH),
+            in_=node_scales_i[SRC_PARTS:P, ALL_NODES : 2 * ALL_NODES]
+            .rearrange("p (b w) -> p b w", b=GRAPHS)
+            .unsqueeze(2)
+            .to_broadcast([P - SRC_PARTS, GRAPHS, TILES_PER_GRAPH, P // 4]),
+        )
+
+        edge_words = edge_sb[:].rearrange("p j e -> p (j e)").bitcast(F32)
+        for j in range(ROW_TILES):
+            grouped = edge_grouped[j // TILES_PER_GRAPH][j % 2]
+            edge_t = psum.tile([P, BANK], F32, tag="bank")
+            planes = edge_t[:, 0 : 2 * P].rearrange("p (u r) -> p u r", u=2)
+            for u in range(2):
+                nc.tensor.transpose(planes[:, u, :], edge_words[:, P * j + u : P * (j + 2) : 2], ident[:])
+            nc.scalar.copy(
+                out=grouped[EDGE_PARTS:P].rearrange("p r t -> p (r t)").bitcast(F32).rearrange("p (r u) -> p r u", u=2),
+                in_=planes[EDGE_PARTS:P].rearrange("p u r -> p r u"),
+            )
+            nc.vector.quantize_mx(
+                out=codes1[:, j, :].bitcast(FP8X4),
+                scales=scales1[:, j, :],
+                in_=grouped[:].rearrange("p r t -> p (r t)"),
+            )
+
+        out_rows = out.flatten_outer_dims()
+        stationary = ((codes0, scales0), (codes1, scales1))
+        for j in range(ROW_TILES):
+            result = results.tile([P, HID], F32)
+            for c in range(COL_TILES):
+                acc = psum.tile([P, BANK], F32, tag="bank")
+                for g in range(PASSES):
+                    codes, scales = stationary[g]
+                    nc.tensor.matmul_mx(
+                        out=acc[:],
+                        lhsT=codes[:, j, :].bitcast(FP8X4),
+                        lhsT_scale=scales[:, j, :],
+                        rhs=w_words[:, g, 2 * BANK * c : 2 * BANK * (c + 1)].bitcast(FP4X4),
+                        rhs_scale=w_scales[:, g, BANK * c : BANK * (c + 1)],
+                        start=(g == 0),
+                        stop=(g == PASSES - 1),
+                    )
+                tenth = tenths.tile([P, BANK], F32)
+                nc.scalar.activation(out=tenth[:], in_=acc[:], func=COPY, scale=NEG_SLOPE)
+                nc.vector.tensor_tensor(out=result[:, BANK * c : BANK * (c + 1)], in0=acc[:], in1=tenth[:], op=MAX)
+            nc.sync.dma_start(out=out_rows[P * j : P * (j + 1), :], in_=result[:])

@@ -40,7 +40,7 @@ def tile_edge_update_only_pa_kernel(tc, node_fts, edge_fts, Wt_words, Wt_scales,
     with ExitStack() as ctx:
         keep = ctx.enter_context(tc.tile_pool(name="keep", bufs=1))
         tenths = ctx.enter_context(tc.tile_pool(name="tenths", bufs=4))
-        results = ctx.enter_context(tc.tile_pool(name="results", bufs=3))
+        results = ctx.enter_context(tc.tile_pool(name="results", bufs=6))
         psum = ctx.enter_context(tc.psum_pool(name="psum", bufs=8))
 
         ident = keep.tile([P, P], F32)

@@ -39,7 +39,7 @@ def tile_edge_update_only_pa_kernel(tc, node_fts, edge_fts, Wt_words, Wt_scales,
     nc = tc.nc
     with ExitStack() as ctx:
         keep = ctx.enter_context(tc.tile_pool(name="keep", bufs=1))
-        tenths = ctx.enter_context(tc.tile_pool(name="tenths", bufs=4))
+        tenths = ctx.enter_context(tc.tile_pool(name="tenths", bufs=8))
         results = ctx.enter_context(tc.tile_pool(name="results", bufs=6))
         psum = ctx.enter_context(tc.psum_pool(name="psum", bufs=8))
 

@@ -23,16 +23,28 @@ NEG_SLOPE = 0.1
 ROWS = GRAPHS * NODES * NODES
 ROW_TILES = ROWS // P
 TILES_PER_GRAPH = ROW_TILES // GRAPHS
+PAIRS = ROW_TILES // 2
 I_PER_TILE = P // NODES
 BANK = 512
 COL_TILES = HID // BANK
 PASSES = 2
 SRC_PARTS = NODE_IN // 4
-EDGE_PARTS = EDGE_IN // 4
+HALF = EDGE_IN // 4
 ALL_NODES = GRAPHS * NODES
 REP = 4
+CODE_WORDS = P
+WORDS = CODE_WORDS + P // 4
+SIZE = 4 * WORDS
 
 FLOPS = 2 * ROWS * (2 * NODE_IN + EDGE_IN) * HID
+
+
+def codes_of(operand):
+    return operand[:, 0 : 4 * CODE_WORDS].bitcast(FP8X4)
+
+
+def scales_of(operand):
+    return operand[:, 4 * CODE_WORDS : SIZE]
 
 
 def tile_edge_update_only_pa_kernel(tc, node_fts, edge_fts, Wt_words, Wt_scales, out):
@@ -40,7 +52,7 @@ def tile_edge_update_only_pa_kernel(tc, node_fts, edge_fts, Wt_words, Wt_scales,
     with ExitStack() as ctx:
         keep = ctx.enter_context(tc.tile_pool(name="keep", bufs=1))
         tenths = ctx.enter_context(tc.tile_pool(name="tenths", bufs=8))
-        results = ctx.enter_context(tc.tile_pool(name="results", bufs=6))
+        results = ctx.enter_context(tc.tile_pool(name="results", bufs=8))
         psum = ctx.enter_context(tc.psum_pool(name="psum", bufs=8))
 
         ident = keep.tile([P, P], F32)
@@ -48,32 +60,46 @@ def tile_edge_update_only_pa_kernel(tc, node_fts, edge_fts, Wt_words, Wt_scales,
         edge_sb = keep.tile([P, ROW_TILES + 1, EDGE_IN], BF16)
         w_words = keep.tile([P, PASSES, 2 * HID], U8, align_bytes=64)
         w_scales = keep.tile([P, PASSES, HID], U8, align_bytes=64)
-        node_grouped = keep.tile([P, 2 * ALL_NODES * REP, 4], BF16, align_bytes=64)
-        node_codes = keep.tile([P, 2 * ALL_NODES * REP], U32, align_bytes=64)
-        node_scales = keep.tile([P, 2 * ALL_NODES * REP], U8, align_bytes=64)
-        codes0 = keep.tile([P, ROW_TILES, P], U32, align_bytes=64)
-        scales0 = keep.tile([P, ROW_TILES, P], U8, align_bytes=64)
-        codes1 = keep.tile([P, ROW_TILES, P], U32, align_bytes=64)
-        scales1 = keep.tile([P, ROW_TILES, P], U8, align_bytes=64)
-        edge_grouped = [
-            [keep.tile([P, P, 4], BF16, name="edge_grouped_%d_%d" % (b, s), align_bytes=64) for s in range(2)]
-            for b in range(GRAPHS)
-        ]
+        src_grouped = keep.tile([P, ALL_NODES * REP, 4], BF16, align_bytes=64)
+        src_codes = keep.tile([P, ALL_NODES * REP], U32, align_bytes=64)
+        src_scales = keep.tile([P, ALL_NODES * REP], U8, align_bytes=64)
+        dst_grouped = keep.tile([P, GRAPHS, P, 4], BF16, align_bytes=64)
+        first_grouped = keep.tile([P, P, 4], BF16, align_bytes=64)
+        dst1_grouped = keep.tile([P, P, 4], BF16, align_bytes=64)
+        pair_grouped = keep.tile([P, PAIRS, P, 4], BF16, align_bytes=64)
+        op0 = keep.tile([P, ROW_TILES, SIZE], U8, align_bytes=64)
+        op1 = keep.tile([P, ROW_TILES, SIZE], U8, align_bytes=64)
+        pair_ops = keep.tile([P, PAIRS, SIZE], U8, align_bytes=64)
+        dst_ops = keep.tile([P, GRAPHS, SIZE], U8, align_bytes=64)
+        dst1_op = keep.tile([P, SIZE], U8, align_bytes=64)
+        op0_i = op0[:].bitcast(I32)
+        op1_i = op1[:].bitcast(I32)
+        pair_i = pair_ops[:].bitcast(I32)
+        dst_i = dst_ops[:].bitcast(I32)
+        dst1_i = dst1_op[:].bitcast(I32)
 
         nc.vector.memset(w_scales[:].rearrange("p g n -> p (g n)").bitcast(I32), 0)
-        nc.vector.memset(node_scales[:].bitcast(I32), 0)
-        nc.gpsimd.memset(nodes2[ALL_NODES:P], 0.0)
-        nc.gpsimd.memset(edge_sb[:, 0, :], 0.0)
+        nc.vector.memset(src_scales[:].bitcast(I32), 0)
+        nc.gpsimd.memset(edge_sb[:, 0, :].bitcast(F32), 0.0)
+        nc.gpsimd.memset(nodes2[ALL_NODES:P].rearrange("p c f -> p (c f)").bitcast(F32), 0.0)
         make_identity(nc, ident[:])
+        nc.gpsimd.memset(dst_i[:, :, CODE_WORDS:WORDS], 0)
+        nc.gpsimd.memset(op1_i[:, 0, CODE_WORDS:WORDS], 0)
+        nc.gpsimd.memset(pair_i[:, :, CODE_WORDS:WORDS], 0)
+        nc.gpsimd.memset(dst1_i[:, CODE_WORDS:WORDS], 0)
+        nc.gpsimd.memset(dst1_grouped[HALF:P].rearrange("p r t -> p (r t)").bitcast(F32), 0.0)
 
-        node_rows = node_fts.flatten_outer_dims()
         nc.scalar.dma_start(
             out=nodes2[0:ALL_NODES],
-            in_=node_rows.unsqueeze(1).to_broadcast([ALL_NODES, 2, NODE_IN]),
+            in_=node_fts.flatten_outer_dims().unsqueeze(1).to_broadcast([ALL_NODES, 2, NODE_IN]),
         )
         edge_rows = edge_fts.flatten_outer_dims().rearrange("(j r) e -> r j e", r=P)
-        for q in range(4):
-            nc.sync.dma_start(out=edge_sb[:, 1 + 4 * q : 5 + 4 * q, :], in_=edge_rows[:, 4 * q : 4 * q + 4, :])
+
+        def load_edges(lo, hi):
+            nc.sync.dma_start(out=edge_sb[:, 1 + lo : 1 + hi, :], in_=edge_rows[:, lo:hi, :])
+
+        load_edges(0, 4)
+        load_edges(4, 8)
         for q in range(4):
             nc.sync.dma_start(
                 out=w_scales[32 * q : 32 * q + 4].bitcast(I32),
@@ -81,29 +107,55 @@ def tile_edge_update_only_pa_kernel(tc, node_fts, edge_fts, Wt_words, Wt_scales,
             )
         for g in range(PASSES):
             nc.sync.dma_start(out=w_words[:, g, :].bitcast(I32), in_=Wt_words[g].bitcast(I32))
+        load_edges(8, 16)
 
         node_words = nodes2[:].rearrange("p c f -> p (c f)").bitcast(F32)
-        first_t = psum.tile([P, BANK], F32, tag="bank")
-        second_t = psum.tile([P, BANK], F32, tag="bank")
-        first_planes = first_t[:, 0 : 2 * P].rearrange("p (u n) -> p u n", u=2)
-        second_planes = second_t[:, 0 : 2 * P].rearrange("p (u n) -> p u n", u=2)
-        for u in range(2):
-            nc.tensor.transpose(first_planes[:, u, :], node_words[:, u : 2 * P : 2], ident[:])
-        for u in range(2):
-            nc.tensor.transpose(second_planes[:, u, :], node_words[:, 64 + u : 64 + 2 * P : 2], ident[:])
+        edge_words = edge_sb[:].rearrange("p j e -> p (j e)").bitcast(F32)
 
-        grouped_words = node_grouped[:].rearrange("p c t -> p (c t)").bitcast(F32)
-        half = 2 * ALL_NODES * REP
-        nc.vector.tensor_copy(
-            out=grouped_words[:, 0:half].rearrange("p (n r u) -> p n r u", r=REP, u=2),
-            in_=first_planes[:, :, 0:ALL_NODES]
-            .rearrange("p u n -> p n u")
-            .unsqueeze(2)
-            .to_broadcast([P, ALL_NODES, REP, 2]),
-        )
-        for b in range(GRAPHS):
+        def transposed(planes, words, first):
+            for u in range(2):
+                nc.tensor.transpose(planes[:, u, :], words[:, first + u : first + 2 * P : 2], ident[:])
+
+        def two_planes(lo, bank_tile):
+            return bank_tile[:, lo : lo + 2 * P].rearrange("p (u r) -> p u r", u=2)
+
+        def regrouped(t):
+            return t.rearrange("p r t -> p (r t)").bitcast(F32).rearrange("p (r u) -> p r u", u=2)
+
+        def pair_planes(first, last):
+            planes = {}
+            for q in range(first, last):
+                if (q - first) % 2 == 0:
+                    bank_tile = psum.tile([P, BANK], F32, tag="bank")
+                planes[q] = two_planes(2 * P * ((q - first) % 2), bank_tile)
+                transposed(planes[q], edge_words, P * (2 * q + 1))
+            return planes
+
+        def dst_of_pass1(grouped, b):
+            nc.scalar.copy(
+                out=grouped[0:HALF].rearrange("p r t -> p (r t)").bitcast(F32).rearrange(
+                    "p (i k u) -> p i k u", i=I_PER_TILE, u=2
+                ),
+                in_=second_planes[0:HALF, :, NODES * b : NODES * (b + 1)]
+                .rearrange("p u k -> p k u")
+                .unsqueeze(1)
+                .to_broadcast([HALF, I_PER_TILE, NODES, 2]),
+            )
+
+        def quantise(operand, grouped):
+            nc.vector.quantize_mx(
+                out=codes_of(operand), scales=scales_of(operand), in_=grouped.rearrange("p r t -> p (r t)")
+            )
+
+        def pair_copy(q, planes):
+            nc.scalar.copy(out=regrouped(pair_grouped[:, q]), in_=planes[q].rearrange("p u r -> p r u"))
+
+        def pair_quantise(q):
+            quantise(pair_ops[:, q, :], pair_grouped[:, q])
+
+        def dst_of_pass0(b):
             nc.vector.tensor_copy(
-                out=grouped_words[:, half + 2 * P * b : half + 2 * P * (b + 1)].rearrange(
+                out=dst_grouped[:, b].rearrange("p r t -> p (r t)").bitcast(F32).rearrange(
                     "p (i k u) -> p i k u", i=I_PER_TILE, u=2
                 ),
                 in_=first_planes[:, :, NODES * b : NODES * (b + 1)]
@@ -111,80 +163,48 @@ def tile_edge_update_only_pa_kernel(tc, node_fts, edge_fts, Wt_words, Wt_scales,
                 .unsqueeze(1)
                 .to_broadcast([P, I_PER_TILE, NODES, 2]),
             )
-            for s in range(2):
-                nc.scalar.copy(
-                    out=edge_grouped[b][s][0:EDGE_PARTS]
-                    .rearrange("p r t -> p (r t)")
-                    .bitcast(F32)
-                    .rearrange("p (i k u) -> p i k u", i=I_PER_TILE, u=2),
-                    in_=second_planes[0:EDGE_PARTS, :, NODES * b : NODES * (b + 1)]
-                    .rearrange("p u k -> p k u")
-                    .unsqueeze(1)
-                    .to_broadcast([EDGE_PARTS, I_PER_TILE, NODES, 2]),
+
+        src_codes_i = src_codes[:].bitcast(I32)
+        src_scales_i = src_scales[:].bitcast(I32)
+
+        def spread_src(lo, hi):
+            nodes_of = slice(I_PER_TILE * lo, I_PER_TILE * hi)
+            for first, source in (
+                (0, src_codes_i[0:SRC_PARTS, REP * I_PER_TILE * lo : REP * I_PER_TILE * hi : REP]),
+                (CODE_WORDS, src_scales_i[0:SRC_PARTS, nodes_of]),
+            ):
+                width = (CODE_WORDS if first == 0 else WORDS - CODE_WORDS) // I_PER_TILE
+                nc.vector.tensor_copy(
+                    out=op0_i[0:SRC_PARTS, lo:hi, first : first + I_PER_TILE * width].rearrange(
+                        "p j (i k) -> p j i k", i=I_PER_TILE
+                    ),
+                    in_=source.rearrange("p (j i) -> p j i", i=I_PER_TILE)
+                    .unsqueeze(3)
+                    .to_broadcast([SRC_PARTS, hi - lo, I_PER_TILE, width]),
                 )
-        nc.vector.quantize_mx(
-            out=node_codes[:].bitcast(FP8X4),
-            scales=node_scales[:],
-            in_=node_grouped[:].rearrange("p c t -> p (c t)"),
-        )
 
-        node_codes_i = node_codes[:].bitcast(I32)
-        node_scales_i = node_scales[:].bitcast(I32)
-        codes0_i = codes0[:].bitcast(I32)
-        scales0_i = scales0[:].rearrange("p j c -> p (j c)").bitcast(I32)
-        n_src = ALL_NODES * REP
-        nc.vector.tensor_copy(
-            out=codes0_i[0:SRC_PARTS].rearrange("p j (i k) -> p (j i) k", k=NODES),
-            in_=node_codes_i[0:SRC_PARTS, 0:n_src:REP].unsqueeze(2).to_broadcast([SRC_PARTS, ALL_NODES, NODES]),
-        )
-        nc.vector.tensor_copy(
-            out=scales0_i[0:SRC_PARTS].rearrange("p (n w) -> p n w", w=NODES // 4),
-            in_=node_scales_i[0:SRC_PARTS, 0:ALL_NODES].unsqueeze(2).to_broadcast([SRC_PARTS, ALL_NODES, NODES // 4]),
-        )
-        nc.vector.tensor_copy(
-            out=codes0_i[SRC_PARTS:P].rearrange("p (b g) c -> p b g c", b=GRAPHS),
-            in_=node_codes_i[SRC_PARTS:P, n_src : 2 * n_src]
-            .rearrange("p (b c) -> p b c", b=GRAPHS)
-            .unsqueeze(2)
-            .to_broadcast([P - SRC_PARTS, GRAPHS, TILES_PER_GRAPH, P]),
-        )
-        nc.vector.tensor_copy(
-            out=scales0_i[SRC_PARTS:P].rearrange("p (b g w) -> p b g w", b=GRAPHS, g=TILES_PER_GRAPH),
-            in_=node_scales_i[SRC_PARTS:P, ALL_NODES : 2 * ALL_NODES]
-            .rearrange("p (b w) -> p b w", b=GRAPHS)
-            .unsqueeze(2)
-            .to_broadcast([P - SRC_PARTS, GRAPHS, TILES_PER_GRAPH, P // 4]),
-        )
+        def move(out_view, in_view):
+            nc.sync.dma_start(out=out_view, in_=in_view)
 
-        edge_words = edge_sb[:].rearrange("p j e -> p (j e)").bitcast(F32)
-        for j in range(ROW_TILES):
-            grouped = edge_grouped[j // TILES_PER_GRAPH][j % 2]
-            edge_t = psum.tile([P, BANK], F32, tag="bank")
-            planes = edge_t[:, 0 : 2 * P].rearrange("p (u r) -> p u r", u=2)
-            for u in range(2):
-                nc.tensor.transpose(planes[:, u, :], edge_words[:, P * j + u : P * (j + 2) : 2], ident[:])
-            nc.scalar.copy(
-                out=grouped[EDGE_PARTS:P].rearrange("p r t -> p (r t)").bitcast(F32).rearrange("p (r u) -> p r u", u=2),
-                in_=planes[EDGE_PARTS:P].rearrange("p u r -> p r u"),
-            )
-            nc.vector.quantize_mx(
-                out=codes1[:, j, :].bitcast(FP8X4),
-                scales=scales1[:, j, :],
-                in_=grouped[:].rearrange("p r t -> p (r t)"),
-            )
+        def edge_moves(first, last):
+            tiles = slice(2 * first, 2 * last)
+            pair_tiles = op1_i[HALF:P, tiles, :].rearrange("p (q e) w -> p q e w", e=2)
+            if first > 0:
+                move(pair_tiles[:, :, 0, :], pair_i[0:HALF, first:last, :])
+            move(pair_tiles[:, :, 1, :], pair_i[HALF:P, first:last, :])
 
         out_rows = out.flatten_outer_dims()
-        stationary = ((codes0, scales0), (codes1, scales1))
-        for j in range(ROW_TILES):
+
+        def row_tile(j):
             result = results.tile([P, HID], F32)
             for c in range(COL_TILES):
                 acc = psum.tile([P, BANK], F32, tag="bank")
                 for g in range(PASSES):
-                    codes, scales = stationary[g]
+                    operand = (op0, op1)[g][:, j, :]
                     nc.tensor.matmul_mx(
                         out=acc[:],
-                        lhsT=codes[:, j, :].bitcast(FP8X4),
-                        lhsT_scale=scales[:, j, :],
+                        lhsT=codes_of(operand),
+                        lhsT_scale=scales_of(operand),
                         rhs=w_words[:, g, 2 * BANK * c : 2 * BANK * (c + 1)].bitcast(FP4X4),
                         rhs_scale=w_scales[:, g, BANK * c : BANK * (c + 1)],
                         start=(g == 0),
@@ -194,3 +214,72 @@ def tile_edge_update_only_pa_kernel(tc, node_fts, edge_fts, Wt_words, Wt_scales,
                 nc.scalar.activation(out=tenth[:], in_=acc[:], func=COPY, scale=NEG_SLOPE)
                 nc.vector.tensor_tensor(out=result[:, BANK * c : BANK * (c + 1)], in0=acc[:], in1=tenth[:], op=MAX)
             nc.sync.dma_start(out=out_rows[P * j : P * (j + 1), :], in_=result[:])
+
+        with tc.manual_schedule(engines={mybir.EngineType.PE, mybir.EngineType.Activation, mybir.EngineType.DVE}):
+            first_t = psum.tile([P, BANK], F32, tag="bank")
+            second_t = psum.tile([P, BANK], F32, tag="bank")
+            first_planes = two_planes(0, first_t)
+            second_planes = two_planes(0, second_t)
+            transposed(first_planes, node_words, 0)
+            transposed(second_planes, node_words, HALF)
+            tile0_t = psum.tile([P, BANK], F32, tag="bank")
+            tile0_planes = two_planes(0, tile0_t)
+            transposed(tile0_planes, edge_words, 0)
+            planes = pair_planes(0, 4)
+
+            nc.vector.tensor_copy(
+                out=src_grouped[:].rearrange("p c t -> p (c t)").bitcast(F32).rearrange(
+                    "p (n r u) -> p n r u", r=REP, u=2
+                ),
+                in_=first_planes[:, :, 0:ALL_NODES]
+                .rearrange("p u n -> p n u")
+                .unsqueeze(2)
+                .to_broadcast([P, ALL_NODES, REP, 2]),
+            )
+            dst_of_pass0(0)
+            dst_of_pass1(first_grouped, 0)
+            nc.scalar.copy(
+                out=regrouped(first_grouped[HALF:P]), in_=tile0_planes[HALF:P].rearrange("p u r -> p r u")
+            )
+            pair_copy(0, planes)
+            pair_copy(1, planes)
+            dst_of_pass1(dst1_grouped, 1)
+            pair_copy(2, planes)
+            pair_copy(3, planes)
+
+            nc.vector.quantize_mx(
+                out=src_codes[:].bitcast(FP8X4), scales=src_scales[:], in_=src_grouped[:].rearrange("p c t -> p (c t)")
+            )
+            quantise(dst_ops[:, 0, :], dst_grouped[:, 0])
+            quantise(op1[:, 0, :], first_grouped[:])
+            move(op1_i[0:HALF, 1:8, :], op1_i[0:HALF, 0:1, :].to_broadcast([HALF, 7, WORDS]))
+            pair_quantise(0)
+            pair_quantise(1)
+            edge_moves(0, 1)
+            spread_src(0, 2)
+            nc.vector.tensor_copy(
+                out=op0_i[SRC_PARTS:P, 0:2, :],
+                in_=dst_i[SRC_PARTS:P, 0:1, :].to_broadcast([P - SRC_PARTS, 2, WORDS]),
+            )
+            move(op0_i[SRC_PARTS:P, 2:8, :], dst_i[SRC_PARTS:P, 0:1, :].to_broadcast([P - SRC_PARTS, 6, WORDS]))
+            dst_of_pass0(1)
+            pair_quantise(2)
+            pair_quantise(3)
+            edge_moves(1, 4)
+            quantise(dst1_op[:], dst1_grouped[:])
+            quantise(dst_ops[:, 1, :], dst_grouped[:, 1])
+            move(op1_i[0:HALF, 8:16, :], dst1_i[0:HALF].unsqueeze(1).to_broadcast([HALF, 8, WORDS]))
+            move(op0_i[SRC_PARTS:P, 8:16, :], dst_i[SRC_PARTS:P, 1:2, :].to_broadcast([P - SRC_PARTS, 8, WORDS]))
+            spread_src(2, 8)
+
+            row_tile(0)
+            row_tile(1)
+            planes = pair_planes(4, 8)
+            for q in range(4, 8):
+                pair_copy(q, planes)
+            for q in range(4, 8):
+                pair_quantise(q)
+            spread_src(8, 16)
+            edge_moves(4, 8)
+            for j in range(2, ROW_TILES):
+                row_tile(j)

@@ -32,19 +32,10 @@ SRC_PARTS = NODE_IN // 4
 HALF = EDGE_IN // 4
 ALL_NODES = GRAPHS * NODES
 REP = 4
-CODE_WORDS = P
-WORDS = CODE_WORDS + P // 4
-SIZE = 4 * WORDS
+SCALE_WORDS = P // 4
+PAIRS_PER_GRAPH = PAIRS // GRAPHS
 
 FLOPS = 2 * ROWS * (2 * NODE_IN + EDGE_IN) * HID
-
-
-def codes_of(operand):
-    return operand[:, 0 : 4 * CODE_WORDS].bitcast(FP8X4)
-
-
-def scales_of(operand):
-    return operand[:, 4 * CODE_WORDS : SIZE]
 
 
 def tile_edge_update_only_pa_kernel(tc, node_fts, edge_fts, Wt_words, Wt_scales, out):
@@ -67,26 +58,34 @@ def tile_edge_update_only_pa_kernel(tc, node_fts, edge_fts, Wt_words, Wt_scales,
         first_grouped = keep.tile([P, P, 4], BF16, align_bytes=64)
         dst1_grouped = keep.tile([P, P, 4], BF16, align_bytes=64)
         pair_grouped = keep.tile([P, PAIRS, P, 4], BF16, align_bytes=64)
-        op0 = keep.tile([P, ROW_TILES, SIZE], U8, align_bytes=64)
-        op1 = keep.tile([P, ROW_TILES, SIZE], U8, align_bytes=64)
-        pair_ops = keep.tile([P, PAIRS, SIZE], U8, align_bytes=64)
-        dst_ops = keep.tile([P, GRAPHS, SIZE], U8, align_bytes=64)
-        dst1_op = keep.tile([P, SIZE], U8, align_bytes=64)
-        op0_i = op0[:].bitcast(I32)
-        op1_i = op1[:].bitcast(I32)
-        pair_i = pair_ops[:].bitcast(I32)
-        dst_i = dst_ops[:].bitcast(I32)
-        dst1_i = dst1_op[:].bitcast(I32)
+        codes0 = keep.tile([P, ROW_TILES, P], U32, align_bytes=64)
+        scales0 = keep.tile([P, ROW_TILES, P], U8, align_bytes=64)
+        codes1 = keep.tile([P, GRAPHS, 2, PAIRS_PER_GRAPH, P], U32, align_bytes=64)
+        scales1 = keep.tile([P, GRAPHS, 2, PAIRS_PER_GRAPH, P], U8, align_bytes=64)
+        pair_codes = keep.tile([P, PAIRS, P], U32, align_bytes=64)
+        pair_scales = keep.tile([P, PAIRS, P], U8, align_bytes=64)
+        dst_codes = keep.tile([P, GRAPHS, P], U32, align_bytes=64)
+        dst_scales = keep.tile([P, GRAPHS, P], U8, align_bytes=64)
+        dst1_codes = keep.tile([P, P], U32, align_bytes=64)
+        dst1_scales = keep.tile([P, P], U8, align_bytes=64)
+        codes0_i = codes0[:].bitcast(I32)
+        scales0_i = scales0[:].bitcast(I32)
+        codes1_i = codes1[:].bitcast(I32)
+        scales1_i = scales1[:].bitcast(I32)
+        pair_codes_i = pair_codes[:].bitcast(I32)
+        pair_scales_i = pair_scales[:].bitcast(I32)
+        dst_codes_i = dst_codes[:].bitcast(I32)
+        dst_scales_i = dst_scales[:].bitcast(I32)
 
         nc.vector.memset(w_scales[:].rearrange("p g n -> p (g n)").bitcast(I32), 0)
         nc.vector.memset(src_scales[:].bitcast(I32), 0)
         nc.gpsimd.memset(edge_sb[:, 0, :].bitcast(F32), 0.0)
         nc.gpsimd.memset(nodes2[ALL_NODES:P].rearrange("p c f -> p (c f)").bitcast(F32), 0.0)
         make_identity(nc, ident[:])
-        nc.gpsimd.memset(dst_i[:, :, CODE_WORDS:WORDS], 0)
-        nc.gpsimd.memset(op1_i[:, 0, CODE_WORDS:WORDS], 0)
-        nc.gpsimd.memset(pair_i[:, :, CODE_WORDS:WORDS], 0)
-        nc.gpsimd.memset(dst1_i[:, CODE_WORDS:WORDS], 0)
+        nc.gpsimd.memset(dst_scales_i, 0)
+        nc.gpsimd.memset(scales1_i[:, 0, 0, 0, :], 0)
+        nc.gpsimd.memset(pair_scales_i, 0)
+        nc.gpsimd.memset(dst1_scales[:].bitcast(I32), 0)
         nc.gpsimd.memset(dst1_grouped[HALF:P].rearrange("p r t -> p (r t)").bitcast(F32), 0.0)
 
         nc.scalar.dma_start(
@@ -122,6 +121,17 @@ def tile_edge_update_only_pa_kernel(tc, node_fts, edge_fts, Wt_words, Wt_scales,
         def regrouped(t):
             return t.rearrange("p r t -> p (r t)").bitcast(F32).rearrange("p (r u) -> p r u", u=2)
 
+        def warm_tensor(count):
+            unused = psum.tile([P, BANK], F32, tag="bank")
+            for again in range(count):
+                nc.tensor.matmul(
+                    out=unused[:],
+                    lhsT=nodes2[:, 0, 0:P],
+                    rhs=edge_sb[:, 1:3, :].rearrange("p j e -> p (j e)"),
+                    start=True,
+                    stop=True,
+                )
+
         def pair_planes(first, last):
             planes = {}
             for q in range(first, last):
@@ -142,16 +152,14 @@ def tile_edge_update_only_pa_kernel(tc, node_fts, edge_fts, Wt_words, Wt_scales,
                 .to_broadcast([HALF, I_PER_TILE, NODES, 2]),
             )
 
-        def quantise(operand, grouped):
-            nc.vector.quantize_mx(
-                out=codes_of(operand), scales=scales_of(operand), in_=grouped.rearrange("p r t -> p (r t)")
-            )
+        def quantise(codes, scales, grouped):
+            nc.vector.quantize_mx(out=codes.bitcast(FP8X4), scales=scales, in_=grouped.rearrange("p r t -> p (r t)"))
 
         def pair_copy(q, planes):
             nc.scalar.copy(out=regrouped(pair_grouped[:, q]), in_=planes[q].rearrange("p u r -> p r u"))
 
         def pair_quantise(q):
-            quantise(pair_ops[:, q, :], pair_grouped[:, q])
+            quantise(pair_codes[:, q, :], pair_scales[:, q, :], pair_grouped[:, q])
 
         def dst_of_pass0(b):
             nc.vector.tensor_copy(
@@ -169,29 +177,32 @@ def tile_edge_update_only_pa_kernel(tc, node_fts, edge_fts, Wt_words, Wt_scales,
 
         def spread_src(lo, hi):
             nodes_of = slice(I_PER_TILE * lo, I_PER_TILE * hi)
-            for first, source in (
-                (0, src_codes_i[0:SRC_PARTS, REP * I_PER_TILE * lo : REP * I_PER_TILE * hi : REP]),
-                (CODE_WORDS, src_scales_i[0:SRC_PARTS, nodes_of]),
+            for out_i, source in (
+                (codes0_i, src_codes_i[0:SRC_PARTS, REP * I_PER_TILE * lo : REP * I_PER_TILE * hi : REP]),
+                (scales0_i, src_scales_i[0:SRC_PARTS, nodes_of]),
             ):
-                width = (CODE_WORDS if first == 0 else WORDS - CODE_WORDS) // I_PER_TILE
-                nc.vector.tensor_copy(
-                    out=op0_i[0:SRC_PARTS, lo:hi, first : first + I_PER_TILE * width].rearrange(
-                        "p j (i k) -> p j i k", i=I_PER_TILE
-                    ),
-                    in_=source.rearrange("p (j i) -> p j i", i=I_PER_TILE)
-                    .unsqueeze(3)
-                    .to_broadcast([SRC_PARTS, hi - lo, I_PER_TILE, width]),
-                )
+                view = out_i[0:SRC_PARTS, lo:hi, :].rearrange("p j (i k) -> p (j i) k", i=I_PER_TILE)
+                nc.vector.tensor_copy(out=view, in_=source.unsqueeze(2).to_broadcast(list(view.shape)))
 
         def move(out_view, in_view):
             nc.sync.dma_start(out=out_view, in_=in_view)
 
+        def dst_moves_of_pass0(b, lo, hi):
+            for out_i, in_i in ((codes0_i, dst_codes_i), (scales0_i, dst_scales_i)):
+                view = out_i[SRC_PARTS:P, lo:hi, :]
+                move(view, in_i[SRC_PARTS:P, b : b + 1, :].to_broadcast(list(view.shape)))
+
+        def dst_moves_of_pass1(b, first, sources):
+            for out_i, source in zip((codes1_i, scales1_i), sources):
+                view = out_i[0:HALF, b].rearrange("p e q w -> p (e q) w")[:, first:]
+                move(view, source.unsqueeze(1).to_broadcast(list(view.shape)))
+
         def edge_moves(first, last):
-            tiles = slice(2 * first, 2 * last)
-            pair_tiles = op1_i[HALF:P, tiles, :].rearrange("p (q e) w -> p q e w", e=2)
-            if first > 0:
-                move(pair_tiles[:, :, 0, :], pair_i[0:HALF, first:last, :])
-            move(pair_tiles[:, :, 1, :], pair_i[HALF:P, first:last, :])
+            b = first // PAIRS_PER_GRAPH
+            places = slice(first - PAIRS_PER_GRAPH * b, last - PAIRS_PER_GRAPH * b)
+            for e in range(2):
+                for out_i, in_i in ((codes1_i, pair_codes_i), (scales1_i, pair_scales_i)):
+                    move(out_i[HALF:P, b, e, places, :], in_i[HALF * e : HALF * (e + 1), first:last, :])
 
         out_rows = out.flatten_outer_dims()
 
@@ -199,12 +210,17 @@ def tile_edge_update_only_pa_kernel(tc, node_fts, edge_fts, Wt_words, Wt_scales,
             result = results.tile([P, HID], F32)
             for c in range(COL_TILES):
                 acc = psum.tile([P, BANK], F32, tag="bank")
+                place = (j // TILES_PER_GRAPH, j % 2, j % TILES_PER_GRAPH // 2)
+                operands = (
+                    (codes0[:, j, :], scales0[:, j, :]),
+                    (codes1[(slice(0, P),) + place], scales1[(slice(0, P),) + place]),
+                )
                 for g in range(PASSES):
-                    operand = (op0, op1)[g][:, j, :]
+                    codes, scales = operands[g]
                     nc.tensor.matmul_mx(
                         out=acc[:],
-                        lhsT=codes_of(operand),
-                        lhsT_scale=scales_of(operand),
+                        lhsT=codes.bitcast(FP8X4),
+                        lhsT_scale=scales,
                         rhs=w_words[:, g, 2 * BANK * c : 2 * BANK * (c + 1)].bitcast(FP4X4),
                         rhs_scale=w_scales[:, g, BANK * c : BANK * (c + 1)],
                         start=(g == 0),
@@ -213,7 +229,11 @@ def tile_edge_update_only_pa_kernel(tc, node_fts, edge_fts, Wt_words, Wt_scales,
                 tenth = tenths.tile([P, BANK], F32)
                 nc.scalar.activation(out=tenth[:], in_=acc[:], func=COPY, scale=NEG_SLOPE)
                 nc.vector.tensor_tensor(out=result[:, BANK * c : BANK * (c + 1)], in0=acc[:], in1=tenth[:], op=MAX)
-            nc.sync.dma_start(out=out_rows[P * j : P * (j + 1), :], in_=result[:])
+                if j == ROW_TILES - 1:
+                    cols = slice(BANK * c, BANK * (c + 1))
+                    nc.sync.dma_start(out=out_rows[P * j : P * (j + 1), cols], in_=result[:, cols])
+            if j < ROW_TILES - 1:
+                nc.sync.dma_start(out=out_rows[P * j : P * (j + 1), :], in_=result[:])
 
         with tc.manual_schedule(engines={mybir.EngineType.PE, mybir.EngineType.Activation, mybir.EngineType.DVE}):
             first_t = psum.tile([P, BANK], F32, tag="bank")
@@ -250,31 +270,31 @@ def tile_edge_update_only_pa_kernel(tc, node_fts, edge_fts, Wt_words, Wt_scales,
             nc.vector.quantize_mx(
                 out=src_codes[:].bitcast(FP8X4), scales=src_scales[:], in_=src_grouped[:].rearrange("p c t -> p (c t)")
             )
-            quantise(dst_ops[:, 0, :], dst_grouped[:, 0])
-            quantise(op1[:, 0, :], first_grouped[:])
-            move(op1_i[0:HALF, 1:8, :], op1_i[0:HALF, 0:1, :].to_broadcast([HALF, 7, WORDS]))
-            pair_quantise(0)
-            pair_quantise(1)
-            edge_moves(0, 1)
+            quantise(dst_codes[:, 0, :], dst_scales[:, 0, :], dst_grouped[:, 0])
+            quantise(codes1[:, 0, 0, 0, :], scales1[:, 0, 0, 0, :], first_grouped[:])
+            quantise(codes1[:, 0, 1, 0, :], scales1[:, 0, 1, 0, :], pair_grouped[:, 0])
+            dst_moves_of_pass1(0, 1, (codes1_i[0:HALF, 0, 0, 0, :], scales1_i[0:HALF, 0, 0, 0, :]))
             spread_src(0, 2)
-            nc.vector.tensor_copy(
-                out=op0_i[SRC_PARTS:P, 0:2, :],
-                in_=dst_i[SRC_PARTS:P, 0:1, :].to_broadcast([P - SRC_PARTS, 2, WORDS]),
-            )
-            move(op0_i[SRC_PARTS:P, 2:8, :], dst_i[SRC_PARTS:P, 0:1, :].to_broadcast([P - SRC_PARTS, 6, WORDS]))
-            dst_of_pass0(1)
-            pair_quantise(2)
-            pair_quantise(3)
+            for out_i, in_i in ((codes0_i, dst_codes_i), (scales0_i, dst_scales_i)):
+                view = out_i[SRC_PARTS:P, 0:2, :]
+                nc.vector.tensor_copy(out=view, in_=in_i[SRC_PARTS:P, 0:1, :].to_broadcast(list(view.shape)))
+            dst_moves_of_pass0(0, 2, TILES_PER_GRAPH)
+            for q in range(1, 4):
+                pair_quantise(q)
             edge_moves(1, 4)
-            quantise(dst1_op[:], dst1_grouped[:])
-            quantise(dst_ops[:, 1, :], dst_grouped[:, 1])
-            move(op1_i[0:HALF, 8:16, :], dst1_i[0:HALF].unsqueeze(1).to_broadcast([HALF, 8, WORDS]))
-            move(op0_i[SRC_PARTS:P, 8:16, :], dst_i[SRC_PARTS:P, 1:2, :].to_broadcast([P - SRC_PARTS, 8, WORDS]))
+            dst_of_pass0(1)
+            quantise(dst1_codes[:], dst1_scales[:], dst1_grouped[:])
+            quantise(dst_codes[:, 1, :], dst_scales[:, 1, :], dst_grouped[:, 1])
+            dst_moves_of_pass1(1, 0, (dst1_codes[0:HALF].bitcast(I32), dst1_scales[0:HALF].bitcast(I32)))
+            dst_moves_of_pass0(1, TILES_PER_GRAPH, ROW_TILES)
             spread_src(2, 8)
+            warm_tensor(4)
 
             row_tile(0)
             row_tile(1)
-            planes = pair_planes(4, 8)
+            planes = pair_planes(4, 6)
+            warm_tensor(2)
+            planes = dict(list(planes.items()) + list(pair_planes(6, 8).items()))
             for q in range(4, 8):
                 pair_copy(q, planes)
             for q in range(4, 8):

@@ -38,6 +38,14 @@ PAIRS_PER_GRAPH = PAIRS // GRAPHS
 FLOPS = 2 * ROWS * (2 * NODE_IN + EDGE_IN) * HID
 
 
+def place_of(q, e):
+    if q == 0:
+        return e
+    if q < PAIRS_PER_GRAPH:
+        return 2 + (PAIRS_PER_GRAPH - 1) * e + q - 1
+    return TILES_PER_GRAPH + PAIRS_PER_GRAPH * e + q - PAIRS_PER_GRAPH
+
+
 def tile_edge_update_only_pa_kernel(tc, node_fts, edge_fts, Wt_words, Wt_scales, out):
     nc = tc.nc
     with ExitStack() as ctx:
@@ -51,17 +59,17 @@ def tile_edge_update_only_pa_kernel(tc, node_fts, edge_fts, Wt_words, Wt_scales,
         edge_sb = keep.tile([P, ROW_TILES + 1, EDGE_IN], BF16)
         w_words = keep.tile([P, PASSES, 2 * HID], U8, align_bytes=64)
         w_scales = keep.tile([P, PASSES, HID], U8, align_bytes=64)
-        src_grouped = keep.tile([P, ALL_NODES * REP, 4], BF16, align_bytes=64)
+        src_grouped = keep.tile([P, GRAPHS, NODES * REP, 4], BF16, align_bytes=64)
         src_codes = keep.tile([P, ALL_NODES * REP], U32, align_bytes=64)
         src_scales = keep.tile([P, ALL_NODES * REP], U8, align_bytes=64)
         dst_grouped = keep.tile([P, GRAPHS, P, 4], BF16, align_bytes=64)
-        first_grouped = keep.tile([P, P, 4], BF16, align_bytes=64)
+        first_grouped = keep.tile([P, 2, P, 4], BF16, align_bytes=64)
         dst1_grouped = keep.tile([P, P, 4], BF16, align_bytes=64)
         pair_grouped = keep.tile([P, PAIRS, P, 4], BF16, align_bytes=64)
         codes0 = keep.tile([P, ROW_TILES, P], U32, align_bytes=64)
         scales0 = keep.tile([P, ROW_TILES, P], U8, align_bytes=64)
-        codes1 = keep.tile([P, GRAPHS, 2, PAIRS_PER_GRAPH, P], U32, align_bytes=64)
-        scales1 = keep.tile([P, GRAPHS, 2, PAIRS_PER_GRAPH, P], U8, align_bytes=64)
+        codes1 = keep.tile([P, ROW_TILES, P], U32, align_bytes=64)
+        scales1 = keep.tile([P, ROW_TILES, P], U8, align_bytes=64)
         pair_codes = keep.tile([P, PAIRS, P], U32, align_bytes=64)
         pair_scales = keep.tile([P, PAIRS, P], U8, align_bytes=64)
         dst_codes = keep.tile([P, GRAPHS, P], U32, align_bytes=64)
@@ -83,7 +91,7 @@ def tile_edge_update_only_pa_kernel(tc, node_fts, edge_fts, Wt_words, Wt_scales,
         nc.gpsimd.memset(nodes2[ALL_NODES:P].rearrange("p c f -> p (c f)").bitcast(F32), 0.0)
         make_identity(nc, ident[:])
         nc.gpsimd.memset(dst_scales_i, 0)
-        nc.gpsimd.memset(scales1_i[:, 0, 0, 0, :], 0)
+        nc.gpsimd.memset(scales1_i[:, 0, :], 0)
         nc.gpsimd.memset(pair_scales_i, 0)
         nc.gpsimd.memset(dst1_scales[:].bitcast(I32), 0)
         nc.gpsimd.memset(dst1_grouped[HALF:P].rearrange("p r t -> p (r t)").bitcast(F32), 0.0)
@@ -96,17 +104,6 @@ def tile_edge_update_only_pa_kernel(tc, node_fts, edge_fts, Wt_words, Wt_scales,
 
         def load_edges(lo, hi):
             nc.sync.dma_start(out=edge_sb[:, 1 + lo : 1 + hi, :], in_=edge_rows[:, lo:hi, :])
-
-        load_edges(0, 4)
-        load_edges(4, 8)
-        for q in range(4):
-            nc.sync.dma_start(
-                out=w_scales[32 * q : 32 * q + 4].bitcast(I32),
-                in_=Wt_scales[:, 4 * q : 4 * q + 4, :].rearrange("g r n -> r g n").bitcast(I32),
-            )
-        for g in range(PASSES):
-            nc.sync.dma_start(out=w_words[:, g, :].bitcast(I32), in_=Wt_words[g].bitcast(I32))
-        load_edges(8, 16)
 
         node_words = nodes2[:].rearrange("p c f -> p (c f)").bitcast(F32)
         edge_words = edge_sb[:].rearrange("p j e -> p (j e)").bitcast(F32)
@@ -192,17 +189,16 @@ def tile_edge_update_only_pa_kernel(tc, node_fts, edge_fts, Wt_words, Wt_scales,
                 view = out_i[SRC_PARTS:P, lo:hi, :]
                 move(view, in_i[SRC_PARTS:P, b : b + 1, :].to_broadcast(list(view.shape)))
 
-        def dst_moves_of_pass1(b, first, sources):
+        def dst_moves_of_pass1(lo, hi, sources):
             for out_i, source in zip((codes1_i, scales1_i), sources):
-                view = out_i[0:HALF, b].rearrange("p e q w -> p (e q) w")[:, first:]
+                view = out_i[0:HALF, lo:hi, :]
                 move(view, source.unsqueeze(1).to_broadcast(list(view.shape)))
 
         def edge_moves(first, last):
-            b = first // PAIRS_PER_GRAPH
-            places = slice(first - PAIRS_PER_GRAPH * b, last - PAIRS_PER_GRAPH * b)
             for e in range(2):
+                places = slice(place_of(first, e), place_of(last - 1, e) + 1)
                 for out_i, in_i in ((codes1_i, pair_codes_i), (scales1_i, pair_scales_i)):
-                    move(out_i[HALF:P, b, e, places, :], in_i[HALF * e : HALF * (e + 1), first:last, :])
+                    move(out_i[HALF:P, places, :], in_i[HALF * e : HALF * (e + 1), first:last, :])
 
         out_rows = out.flatten_outer_dims()
 
@@ -210,10 +206,10 @@ def tile_edge_update_only_pa_kernel(tc, node_fts, edge_fts, Wt_words, Wt_scales,
             result = results.tile([P, HID], F32)
             for c in range(COL_TILES):
                 acc = psum.tile([P, BANK], F32, tag="bank")
-                place = (j // TILES_PER_GRAPH, j % 2, j % TILES_PER_GRAPH // 2)
+                place = place_of(j // 2, j % 2)
                 operands = (
                     (codes0[:, j, :], scales0[:, j, :]),
-                    (codes1[(slice(0, P),) + place], scales1[(slice(0, P),) + place]),
+                    (codes1[:, place, :], scales1[:, place, :]),
                 )
                 for g in range(PASSES):
                     codes, scales = operands[g]
@@ -235,7 +231,55 @@ def tile_edge_update_only_pa_kernel(tc, node_fts, edge_fts, Wt_words, Wt_scales,
             if j < ROW_TILES - 1:
                 nc.sync.dma_start(out=out_rows[P * j : P * (j + 1), :], in_=result[:])
 
-        with tc.manual_schedule(engines={mybir.EngineType.PE, mybir.EngineType.Activation, mybir.EngineType.DVE}):
+        def prepare_pairs(first, last):
+            planes = {}
+            for q in range(first, last, 2):
+                planes = dict(list(planes.items()) + list(pair_planes(q, q + 2).items()))
+            for q in range(first, last):
+                pair_copy(q, planes)
+            for q in range(first, last):
+                pair_quantise(q)
+            edge_moves(first, last)
+
+        def src_copy(b):
+            nc.vector.tensor_copy(
+                out=src_grouped[:, b].rearrange("p c t -> p (c t)").bitcast(F32).rearrange(
+                    "p (n r u) -> p n r u", r=REP, u=2
+                ),
+                in_=first_planes[:, :, NODES * b : NODES * (b + 1)]
+                .rearrange("p u n -> p n u")
+                .unsqueeze(2)
+                .to_broadcast([P, NODES, REP, 2]),
+            )
+
+        def src_quantise(b):
+            cols = slice(NODES * REP * b, NODES * REP * (b + 1))
+            quantise(src_codes[:, cols], src_scales[:, cols], src_grouped[:, b])
+
+        def load_all_but_last_edges():
+            load_edges(0, 4)
+            for q in range(4):
+                nc.sync.dma_start(
+                    out=w_scales[32 * q : 32 * q + 4].bitcast(I32),
+                    in_=Wt_scales[:, 4 * q : 4 * q + 4, :].rearrange("g r n -> r g n").bitcast(I32),
+                )
+            for h in range(2):
+                cols = slice(HID * h, HID * (h + 1))
+                nc.sync.dma_start(
+                    out=w_words[:, :, cols].bitcast(I32),
+                    in_=Wt_words[:, :, cols].rearrange("g p n -> p g n").bitcast(I32),
+                )
+            load_edges(4, 8)
+
+        with tc.manual_schedule(
+            engines={
+                mybir.EngineType.PE,
+                mybir.EngineType.Activation,
+                mybir.EngineType.DVE,
+                mybir.EngineType.SP,
+            }
+        ):
+            load_all_but_last_edges()
             first_t = psum.tile([P, BANK], F32, tag="bank")
             second_t = psum.tile([P, BANK], F32, tag="bank")
             first_planes = two_planes(0, first_t)
@@ -245,61 +289,46 @@ def tile_edge_update_only_pa_kernel(tc, node_fts, edge_fts, Wt_words, Wt_scales,
             tile0_t = psum.tile([P, BANK], F32, tag="bank")
             tile0_planes = two_planes(0, tile0_t)
             transposed(tile0_planes, edge_words, 0)
-            planes = pair_planes(0, 4)
+            planes = pair_planes(0, 2)
 
-            nc.vector.tensor_copy(
-                out=src_grouped[:].rearrange("p c t -> p (c t)").bitcast(F32).rearrange(
-                    "p (n r u) -> p n r u", r=REP, u=2
-                ),
-                in_=first_planes[:, :, 0:ALL_NODES]
-                .rearrange("p u n -> p n u")
-                .unsqueeze(2)
-                .to_broadcast([P, ALL_NODES, REP, 2]),
-            )
-            dst_of_pass0(0)
-            dst_of_pass1(first_grouped, 0)
-            nc.scalar.copy(
-                out=regrouped(first_grouped[HALF:P]), in_=tile0_planes[HALF:P].rearrange("p u r -> p r u")
-            )
-            pair_copy(0, planes)
+            for j, upper in enumerate((tile0_planes, planes[0])):
+                dst_of_pass1(first_grouped[:, j], 0)
+                nc.scalar.copy(
+                    out=regrouped(first_grouped[HALF:P, j]), in_=upper[HALF:P].rearrange("p u r -> p r u")
+                )
             pair_copy(1, planes)
             dst_of_pass1(dst1_grouped, 1)
-            pair_copy(2, planes)
-            pair_copy(3, planes)
 
-            nc.vector.quantize_mx(
-                out=src_codes[:].bitcast(FP8X4), scales=src_scales[:], in_=src_grouped[:].rearrange("p c t -> p (c t)")
-            )
+            src_copy(0)
+            dst_of_pass0(0)
+            src_quantise(0)
             quantise(dst_codes[:, 0, :], dst_scales[:, 0, :], dst_grouped[:, 0])
-            quantise(codes1[:, 0, 0, 0, :], scales1[:, 0, 0, 0, :], first_grouped[:])
-            quantise(codes1[:, 0, 1, 0, :], scales1[:, 0, 1, 0, :], pair_grouped[:, 0])
-            dst_moves_of_pass1(0, 1, (codes1_i[0:HALF, 0, 0, 0, :], scales1_i[0:HALF, 0, 0, 0, :]))
+            quantise(codes1[:, 0, :], scales1[:, 0, :], first_grouped[:, 0])
             spread_src(0, 2)
             for out_i, in_i in ((codes0_i, dst_codes_i), (scales0_i, dst_scales_i)):
                 view = out_i[SRC_PARTS:P, 0:2, :]
                 nc.vector.tensor_copy(out=view, in_=in_i[SRC_PARTS:P, 0:1, :].to_broadcast(list(view.shape)))
+            quantise(codes1[:, 1, :], scales1[:, 1, :], first_grouped[:, 1])
+            pair_quantise(1)
+            edge_moves(1, 2)
+            dst_moves_of_pass1(2, TILES_PER_GRAPH, (codes1_i[0:HALF, 0, :], scales1_i[0:HALF, 0, :]))
             dst_moves_of_pass0(0, 2, TILES_PER_GRAPH)
-            for q in range(1, 4):
-                pair_quantise(q)
-            edge_moves(1, 4)
+            load_edges(8, 16)
+            src_copy(1)
             dst_of_pass0(1)
+            spread_src(2, 8)
             quantise(dst1_codes[:], dst1_scales[:], dst1_grouped[:])
             quantise(dst_codes[:, 1, :], dst_scales[:, 1, :], dst_grouped[:, 1])
-            dst_moves_of_pass1(1, 0, (dst1_codes[0:HALF].bitcast(I32), dst1_scales[0:HALF].bitcast(I32)))
+            src_quantise(1)
+            dst_moves_of_pass1(TILES_PER_GRAPH, ROW_TILES, (dst1_codes[0:HALF].bitcast(I32), dst1_scales[0:HALF].bitcast(I32)))
             dst_moves_of_pass0(1, TILES_PER_GRAPH, ROW_TILES)
-            spread_src(2, 8)
             warm_tensor(4)
 
             row_tile(0)
+            prepare_pairs(2, 4)
             row_tile(1)
-            planes = pair_planes(4, 6)
-            warm_tensor(2)
-            planes = dict(list(planes.items()) + list(pair_planes(6, 8).items()))
-            for q in range(4, 8):
-                pair_copy(q, planes)
-            for q in range(4, 8):
-                pair_quantise(q)
+            row_tile(2)
+            prepare_pairs(4, 8)
             spread_src(8, 16)
-            edge_moves(4, 8)
-            for j in range(2, ROW_TILES):
+            for j in range(3, ROW_TILES):
                 row_tile(j)

@@ -59,42 +59,37 @@ def tile_edge_update_only_pa_kernel(tc, node_fts, edge_fts, Wt_words, Wt_scales,
         edge_sb = keep.tile([P, ROW_TILES + 1, EDGE_IN], BF16)
         w_words = keep.tile([P, PASSES, 2 * HID], U8, align_bytes=64)
         w_scales = keep.tile([P, PASSES, HID], U8, align_bytes=64)
-        src_grouped = keep.tile([P, GRAPHS, NODES * REP, 4], BF16, align_bytes=64)
-        src_codes = keep.tile([P, ALL_NODES * REP], U32, align_bytes=64)
-        src_scales = keep.tile([P, ALL_NODES * REP], U8, align_bytes=64)
-        dst_grouped = keep.tile([P, GRAPHS, P, 4], BF16, align_bytes=64)
+        head_grouped = keep.tile([P, 2, P, 4], BF16, align_bytes=64)
+        late_grouped = keep.tile([P, 4, P, 4], BF16, align_bytes=64)
+        late_codes = keep.tile([P, 4, P], U32, align_bytes=64)
+        late_scales = keep.tile([P, 4, P], U8, align_bytes=64)
         first_grouped = keep.tile([P, 2, P, 4], BF16, align_bytes=64)
-        dst1_grouped = keep.tile([P, P, 4], BF16, align_bytes=64)
         pair_grouped = keep.tile([P, PAIRS, P, 4], BF16, align_bytes=64)
-        codes0 = keep.tile([P, ROW_TILES, P], U32, align_bytes=64)
-        scales0 = keep.tile([P, ROW_TILES, P], U8, align_bytes=64)
+        codes0 = keep.tile([P, 1 + ROW_TILES, P], U32, align_bytes=64)
+        scales0 = keep.tile([P, 1 + ROW_TILES, P], U8, align_bytes=64)
         codes1 = keep.tile([P, ROW_TILES, P], U32, align_bytes=64)
         scales1 = keep.tile([P, ROW_TILES, P], U8, align_bytes=64)
         pair_codes = keep.tile([P, PAIRS, P], U32, align_bytes=64)
         pair_scales = keep.tile([P, PAIRS, P], U8, align_bytes=64)
-        dst_codes = keep.tile([P, GRAPHS, P], U32, align_bytes=64)
-        dst_scales = keep.tile([P, GRAPHS, P], U8, align_bytes=64)
-        dst1_codes = keep.tile([P, P], U32, align_bytes=64)
-        dst1_scales = keep.tile([P, P], U8, align_bytes=64)
         codes0_i = codes0[:].bitcast(I32)
         scales0_i = scales0[:].bitcast(I32)
         codes1_i = codes1[:].bitcast(I32)
         scales1_i = scales1[:].bitcast(I32)
         pair_codes_i = pair_codes[:].bitcast(I32)
         pair_scales_i = pair_scales[:].bitcast(I32)
-        dst_codes_i = dst_codes[:].bitcast(I32)
-        dst_scales_i = dst_scales[:].bitcast(I32)
+        late_codes_i = late_codes[:].bitcast(I32)
+        late_scales_i = late_scales[:].bitcast(I32)
 
         nc.vector.memset(w_scales[:].rearrange("p g n -> p (g n)").bitcast(I32), 0)
-        nc.vector.memset(src_scales[:].bitcast(I32), 0)
         nc.gpsimd.memset(edge_sb[:, 0, :].bitcast(F32), 0.0)
         nc.gpsimd.memset(nodes2[ALL_NODES:P].rearrange("p c f -> p (c f)").bitcast(F32), 0.0)
         make_identity(nc, ident[:])
-        nc.gpsimd.memset(dst_scales_i, 0)
+        nc.gpsimd.memset(scales0_i[:, 0:2, :], 0)
         nc.gpsimd.memset(scales1_i[:, 0, :], 0)
         nc.gpsimd.memset(pair_scales_i, 0)
-        nc.gpsimd.memset(dst1_scales[:].bitcast(I32), 0)
-        nc.gpsimd.memset(dst1_grouped[HALF:P].rearrange("p r t -> p (r t)").bitcast(F32), 0.0)
+        nc.gpsimd.memset(late_scales_i, 0)
+        nc.gpsimd.memset(late_grouped[HALF:P, 0].rearrange("p r t -> p (r t)").bitcast(F32), 0.0)
+        nc.gpsimd.memset(late_grouped[:, 3].rearrange("p r t -> p (r t)").bitcast(F32), 0.0)
 
         nc.scalar.dma_start(
             out=nodes2[0:ALL_NODES],
@@ -130,12 +125,10 @@ def tile_edge_update_only_pa_kernel(tc, node_fts, edge_fts, Wt_words, Wt_scales,
                 )
 
         def pair_planes(first, last):
-            planes = {}
+            bank_tile = psum.tile([P, BANK], F32, tag="bank")
+            planes = bank_tile[:, 0 : 2 * P * (last - first)].rearrange("p (q u r) -> p q u r", u=2, r=P)
             for q in range(first, last):
-                if (q - first) % 2 == 0:
-                    bank_tile = psum.tile([P, BANK], F32, tag="bank")
-                planes[q] = two_planes(2 * P * ((q - first) % 2), bank_tile)
-                transposed(planes[q], edge_words, P * (2 * q + 1))
+                transposed(planes[:, q - first], edge_words, P * (2 * q + 1))
             return planes
 
         def dst_of_pass1(grouped, b):
@@ -150,17 +143,27 @@ def tile_edge_update_only_pa_kernel(tc, node_fts, edge_fts, Wt_words, Wt_scales,
             )
 
         def quantise(codes, scales, grouped):
-            nc.vector.quantize_mx(out=codes.bitcast(FP8X4), scales=scales, in_=grouped.rearrange("p r t -> p (r t)"))
+            nc.vector.quantize_mx(
+                out=codes.rearrange("p a c -> p (a c)").bitcast(FP8X4),
+                scales=scales.rearrange("p a c -> p (a c)"),
+                in_=grouped.rearrange("p a r t -> p (a r t)"),
+            )
 
-        def pair_copy(q, planes):
-            nc.scalar.copy(out=regrouped(pair_grouped[:, q]), in_=planes[q].rearrange("p u r -> p r u"))
+        def pair_quantise(first, last):
+            quantise(pair_codes[:, first:last], pair_scales[:, first:last], pair_grouped[:, first:last])
 
-        def pair_quantise(q):
-            quantise(pair_codes[:, q, :], pair_scales[:, q, :], pair_grouped[:, q])
+        def pair_copy(first, last, planes):
+            nc.scalar.copy(
+                out=pair_grouped[:, first:last]
+                .rearrange("p q r t -> p (q r t)")
+                .bitcast(F32)
+                .rearrange("p (q r u) -> p q r u", q=last - first, u=2),
+                in_=planes.rearrange("p q u r -> p q r u"),
+            )
 
-        def dst_of_pass0(b):
-            nc.vector.tensor_copy(
-                out=dst_grouped[:, b].rearrange("p r t -> p (r t)").bitcast(F32).rearrange(
+        def dst_of_pass0(copy, grouped, b):
+            copy(
+                out=grouped.rearrange("p r t -> p (r t)").bitcast(F32).rearrange(
                     "p (i k u) -> p i k u", i=I_PER_TILE, u=2
                 ),
                 in_=first_planes[:, :, NODES * b : NODES * (b + 1)]
@@ -169,36 +172,20 @@ def tile_edge_update_only_pa_kernel(tc, node_fts, edge_fts, Wt_words, Wt_scales,
                 .to_broadcast([P, I_PER_TILE, NODES, 2]),
             )
 
-        src_codes_i = src_codes[:].bitcast(I32)
-        src_scales_i = src_scales[:].bitcast(I32)
-
-        def spread_src(lo, hi):
-            nodes_of = slice(I_PER_TILE * lo, I_PER_TILE * hi)
-            for out_i, source in (
-                (codes0_i, src_codes_i[0:SRC_PARTS, REP * I_PER_TILE * lo : REP * I_PER_TILE * hi : REP]),
-                (scales0_i, src_scales_i[0:SRC_PARTS, nodes_of]),
-            ):
-                view = out_i[0:SRC_PARTS, lo:hi, :].rearrange("p j (i k) -> p (j i) k", i=I_PER_TILE)
+        def spread_src(b, codes_i, scales_i):
+            tiles = slice(1 + TILES_PER_GRAPH * b, 1 + TILES_PER_GRAPH * (b + 1))
+            for out_i, source in ((codes0_i, codes_i[0:SRC_PARTS, 0:P:REP]), (scales0_i, scales_i[0:SRC_PARTS])):
+                view = out_i[0:SRC_PARTS, tiles, :].rearrange("p j (i k) -> p (j i) k", i=I_PER_TILE)
                 nc.vector.tensor_copy(out=view, in_=source.unsqueeze(2).to_broadcast(list(view.shape)))
 
-        def move(out_view, in_view):
-            nc.sync.dma_start(out=out_view, in_=in_view)
+        def repeat(copy, out_view, source):
+            copy(out=out_view, in_=source.unsqueeze(1).to_broadcast(list(out_view.shape)))
 
-        def dst_moves_of_pass0(b, lo, hi):
-            for out_i, in_i in ((codes0_i, dst_codes_i), (scales0_i, dst_scales_i)):
-                view = out_i[SRC_PARTS:P, lo:hi, :]
-                move(view, in_i[SRC_PARTS:P, b : b + 1, :].to_broadcast(list(view.shape)))
-
-        def dst_moves_of_pass1(lo, hi, sources):
-            for out_i, source in zip((codes1_i, scales1_i), sources):
-                view = out_i[0:HALF, lo:hi, :]
-                move(view, source.unsqueeze(1).to_broadcast(list(view.shape)))
-
-        def edge_moves(first, last):
-            for e in range(2):
+        def edge_moves(first, last, second_tiles):
+            for e, copy in enumerate((nc.sync.dma_start, second_tiles)):
                 places = slice(place_of(first, e), place_of(last - 1, e) + 1)
                 for out_i, in_i in ((codes1_i, pair_codes_i), (scales1_i, pair_scales_i)):
-                    move(out_i[HALF:P, places, :], in_i[HALF * e : HALF * (e + 1), first:last, :])
+                    copy(out=out_i[HALF:P, places, :], in_=in_i[HALF * e : HALF * (e + 1), first:last, :])
 
         out_rows = out.flatten_outer_dims()
 
@@ -208,7 +195,7 @@ def tile_edge_update_only_pa_kernel(tc, node_fts, edge_fts, Wt_words, Wt_scales,
                 acc = psum.tile([P, BANK], F32, tag="bank")
                 place = place_of(j // 2, j % 2)
                 operands = (
-                    (codes0[:, j, :], scales0[:, j, :]),
+                    (codes0[:, 1 + j, :], scales0[:, 1 + j, :]),
                     (codes1[:, place, :], scales1[:, place, :]),
                 )
                 for g in range(PASSES):
@@ -225,51 +212,34 @@ def tile_edge_update_only_pa_kernel(tc, node_fts, edge_fts, Wt_words, Wt_scales,
                 tenth = tenths.tile([P, BANK], F32)
                 nc.scalar.activation(out=tenth[:], in_=acc[:], func=COPY, scale=NEG_SLOPE)
                 nc.vector.tensor_tensor(out=result[:, BANK * c : BANK * (c + 1)], in0=acc[:], in1=tenth[:], op=MAX)
-                if j == ROW_TILES - 1:
+                if j in (0, ROW_TILES - 1):
                     cols = slice(BANK * c, BANK * (c + 1))
                     nc.sync.dma_start(out=out_rows[P * j : P * (j + 1), cols], in_=result[:, cols])
-            if j < ROW_TILES - 1:
+            if 0 < j < ROW_TILES - 1:
                 nc.sync.dma_start(out=out_rows[P * j : P * (j + 1), :], in_=result[:])
 
         def prepare_pairs(first, last):
-            planes = {}
+            planes = [pair_planes(q, q + 2) for q in range(first, last, 2)]
             for q in range(first, last, 2):
-                planes = dict(list(planes.items()) + list(pair_planes(q, q + 2).items()))
-            for q in range(first, last):
-                pair_copy(q, planes)
-            for q in range(first, last):
-                pair_quantise(q)
-            edge_moves(first, last)
+                pair_copy(q, q + 2, planes[(q - first) // 2])
+            pair_quantise(first, last)
+            edge_moves(first, last, nc.gpsimd.tensor_copy)
 
-        def src_copy(b):
-            nc.vector.tensor_copy(
-                out=src_grouped[:, b].rearrange("p c t -> p (c t)").bitcast(F32).rearrange(
-                    "p (n r u) -> p n r u", r=REP, u=2
-                ),
+        def src_copy(copy, grouped, b):
+            copy(
+                out=grouped.rearrange("p c t -> p (c t)").bitcast(F32).rearrange("p (n r u) -> p n r u", r=REP, u=2),
                 in_=first_planes[:, :, NODES * b : NODES * (b + 1)]
                 .rearrange("p u n -> p n u")
                 .unsqueeze(2)
                 .to_broadcast([P, NODES, REP, 2]),
             )
 
-        def src_quantise(b):
-            cols = slice(NODES * REP * b, NODES * REP * (b + 1))
-            quantise(src_codes[:, cols], src_scales[:, cols], src_grouped[:, b])
-
-        def load_all_but_last_edges():
-            load_edges(0, 4)
-            for q in range(4):
-                nc.sync.dma_start(
-                    out=w_scales[32 * q : 32 * q + 4].bitcast(I32),
-                    in_=Wt_scales[:, 4 * q : 4 * q + 4, :].rearrange("g r n -> r g n").bitcast(I32),
-                )
-            for h in range(2):
-                cols = slice(HID * h, HID * (h + 1))
-                nc.sync.dma_start(
-                    out=w_words[:, :, cols].bitcast(I32),
-                    in_=Wt_words[:, :, cols].rearrange("g p n -> p g n").bitcast(I32),
-                )
-            load_edges(4, 8)
+        def load_weights(h):
+            cols = slice(HID * h, HID * (h + 1))
+            nc.sync.dma_start(
+                out=w_words[:, :, cols].bitcast(I32),
+                in_=Wt_words[:, :, cols].rearrange("g p n -> p g n").bitcast(I32),
+            )
 
         with tc.manual_schedule(
             engines={
@@ -277,9 +247,19 @@ def tile_edge_update_only_pa_kernel(tc, node_fts, edge_fts, Wt_words, Wt_scales,
                 mybir.EngineType.Activation,
                 mybir.EngineType.DVE,
                 mybir.EngineType.SP,
+                mybir.EngineType.Pool,
             }
         ):
-            load_all_but_last_edges()
+            load_edges(0, 4)
+            for q in range(4):
+                nc.sync.dma_start(
+                    out=w_scales[32 * q : 32 * q + 4].bitcast(I32),
+                    in_=Wt_scales[:, 4 * q : 4 * q + 4, :].rearrange("g r n -> r g n").bitcast(I32),
+                )
+            load_weights(0)
+            load_weights(1)
+            load_edges(4, 8)
+
             first_t = psum.tile([P, BANK], F32, tag="bank")
             second_t = psum.tile([P, BANK], F32, tag="bank")
             first_planes = two_planes(0, first_t)
@@ -291,37 +271,32 @@ def tile_edge_update_only_pa_kernel(tc, node_fts, edge_fts, Wt_words, Wt_scales,
             transposed(tile0_planes, edge_words, 0)
             planes = pair_planes(0, 2)
 
-            for j, upper in enumerate((tile0_planes, planes[0])):
+            for j, upper in enumerate((tile0_planes, planes[:, 0])):
                 dst_of_pass1(first_grouped[:, j], 0)
                 nc.scalar.copy(
                     out=regrouped(first_grouped[HALF:P, j]), in_=upper[HALF:P].rearrange("p u r -> p r u")
                 )
-            pair_copy(1, planes)
-            dst_of_pass1(dst1_grouped, 1)
+            pair_copy(1, 2, planes[:, 1:2])
+            dst_of_pass1(late_grouped[:, 0], 1)
 
-            src_copy(0)
-            dst_of_pass0(0)
-            src_quantise(0)
-            quantise(dst_codes[:, 0, :], dst_scales[:, 0, :], dst_grouped[:, 0])
-            quantise(codes1[:, 0, :], scales1[:, 0, :], first_grouped[:, 0])
-            spread_src(0, 2)
-            for out_i, in_i in ((codes0_i, dst_codes_i), (scales0_i, dst_scales_i)):
-                view = out_i[SRC_PARTS:P, 0:2, :]
-                nc.vector.tensor_copy(out=view, in_=in_i[SRC_PARTS:P, 0:1, :].to_broadcast(list(view.shape)))
-            quantise(codes1[:, 1, :], scales1[:, 1, :], first_grouped[:, 1])
-            pair_quantise(1)
-            edge_moves(1, 2)
-            dst_moves_of_pass1(2, TILES_PER_GRAPH, (codes1_i[0:HALF, 0, :], scales1_i[0:HALF, 0, :]))
-            dst_moves_of_pass0(0, 2, TILES_PER_GRAPH)
+            src_copy(nc.vector.tensor_copy, head_grouped[:, 0], 0)
+            dst_of_pass0(nc.vector.tensor_copy, head_grouped[:, 1], 0)
+            src_copy(nc.scalar.copy, late_grouped[:, 1], 1)
+            dst_of_pass0(nc.scalar.copy, late_grouped[:, 2], 1)
+            quantise(codes0[:, 0:2], scales0[:, 0:2], head_grouped[:])
+            quantise(codes1[:, 0:1], scales1[:, 0:1], first_grouped[:, 0:1])
+            spread_src(0, codes0_i[:, 0, :], scales0_i[:, 0, :])
+            nc.vector.tensor_copy(out=codes0_i[SRC_PARTS:P, 2, :], in_=codes0_i[SRC_PARTS:P, 1, :])
+            repeat(nc.vector.tensor_copy, scales0_i[SRC_PARTS:P, 2:9, :], scales0_i[SRC_PARTS:P, 1, :])
+            repeat(nc.vector.tensor_copy, scales1_i[0:HALF, 2:8, :], scales1_i[0:HALF, 0, :])
+            quantise(codes1[:, 1:2], scales1[:, 1:2], first_grouped[:, 1:2])
+            pair_quantise(1, 2)
+            edge_moves(1, 2, nc.sync.dma_start)
+            repeat(nc.sync.dma_start, codes1_i[0:HALF, 2:8, :], codes1_i[0:HALF, 0, :])
+            repeat(nc.sync.dma_start, codes0_i[SRC_PARTS:P, 3:9, :], codes0_i[SRC_PARTS:P, 1, :])
             load_edges(8, 16)
-            src_copy(1)
-            dst_of_pass0(1)
-            spread_src(2, 8)
-            quantise(dst1_codes[:], dst1_scales[:], dst1_grouped[:])
-            quantise(dst_codes[:, 1, :], dst_scales[:, 1, :], dst_grouped[:, 1])
-            src_quantise(1)
-            dst_moves_of_pass1(TILES_PER_GRAPH, ROW_TILES, (dst1_codes[0:HALF].bitcast(I32), dst1_scales[0:HALF].bitcast(I32)))
-            dst_moves_of_pass0(1, TILES_PER_GRAPH, ROW_TILES)
+            quantise(late_codes[:], late_scales[:], late_grouped[:])
+            spread_src(1, late_codes_i[:, 1, :], late_scales_i[:, 1, :])
             warm_tensor(4)
 
             row_tile(0)
@@ -329,6 +304,12 @@ def tile_edge_update_only_pa_kernel(tc, node_fts, edge_fts, Wt_words, Wt_scales,
             row_tile(1)
             row_tile(2)
             prepare_pairs(4, 8)
-            spread_src(8, 16)
+            for tile in (8, 12):
+                for first, ops, parts, slot in (
+                    (tile, (codes1_i, scales1_i), slice(0, HALF), 0),
+                    (1 + tile, (codes0_i, scales0_i), slice(SRC_PARTS, P), 2),
+                ):
+                    for out_i, source in zip(ops, (late_codes_i, late_scales_i)):
+                        repeat(nc.gpsimd.tensor_copy, out_i[parts, first : first + 4, :], source[parts, slot, :])
             for j in range(3, ROW_TILES):
                 row_tile(j)

from contextlib import ExitStack

import concourse.mybir as mybir
from concourse.masks import make_identity

F32 = mybir.dt.float32
BF16 = mybir.dt.bfloat16
I32 = mybir.dt.int32
U32 = mybir.dt.uint32
U8 = mybir.dt.uint8
FP8X4 = mybir.dt.float8_e4m3fn_x4
FP4X4 = mybir.dt.float4_e2m1fn_x4
COPY = mybir.ActivationFunctionType.Copy
MAX = mybir.AluOpType.max

P = 128
GRAPHS = 2
NODES = 32
NODE_IN = 384
EDGE_IN = 256
HID = 2048
NEG_SLOPE = 0.1
ROWS = GRAPHS * NODES * NODES
ROW_TILES = ROWS // P
TILES_PER_GRAPH = ROW_TILES // GRAPHS
PAIRS = ROW_TILES // 2
I_PER_TILE = P // NODES
BANK = 512
COL_TILES = HID // BANK
PASSES = 2
SRC_PARTS = NODE_IN // 4
HALF = EDGE_IN // 4
ALL_NODES = GRAPHS * NODES
REP = 4
SCALE_WORDS = P // 4
PAIRS_PER_GRAPH = PAIRS // GRAPHS

FLOPS = 2 * ROWS * (2 * NODE_IN + EDGE_IN) * HID


def place_of(q, e):
    if q == 0:
        return e
    if q < PAIRS_PER_GRAPH:
        return 2 + (PAIRS_PER_GRAPH - 1) * e + q - 1
    return TILES_PER_GRAPH + PAIRS_PER_GRAPH * e + q - PAIRS_PER_GRAPH


def tile_edge_update_only_pa_kernel(tc, node_fts, edge_fts, Wt_words, Wt_scales, out):
    nc = tc.nc
    with ExitStack() as ctx:
        keep = ctx.enter_context(tc.tile_pool(name="keep", bufs=1))
        tenths = ctx.enter_context(tc.tile_pool(name="tenths", bufs=8))
        results = ctx.enter_context(tc.tile_pool(name="results", bufs=8))
        psum = ctx.enter_context(tc.psum_pool(name="psum", bufs=8))

        ident = keep.tile([P, P], F32)
        nodes2 = keep.tile([P, 2, NODE_IN], BF16)
        edge_sb = keep.tile([P, ROW_TILES + 1, EDGE_IN], BF16)
        w_words = keep.tile([P, PASSES, 2 * HID], U8, align_bytes=64)
        w_scales = keep.tile([P, PASSES, HID], U8, align_bytes=64)
        head_grouped = keep.tile([P, 2, P, 4], BF16, align_bytes=64)
        late_grouped = keep.tile([P, 4, P, 4], BF16, align_bytes=64)
        late_codes = keep.tile([P, 4, P], U32, align_bytes=64)
        late_scales = keep.tile([P, 4, P], U8, align_bytes=64)
        first_grouped = keep.tile([P, 2, P, 4], BF16, align_bytes=64)
        pair_grouped = keep.tile([P, PAIRS, P, 4], BF16, align_bytes=64)
        codes0 = keep.tile([P, 1 + ROW_TILES, P], U32, align_bytes=64)
        scales0 = keep.tile([P, 1 + ROW_TILES, P], U8, align_bytes=64)
        codes1 = keep.tile([P, ROW_TILES, P], U32, align_bytes=64)
        scales1 = keep.tile([P, ROW_TILES, P], U8, align_bytes=64)
        pair_codes = keep.tile([P, PAIRS, P], U32, align_bytes=64)
        pair_scales = keep.tile([P, PAIRS, P], U8, align_bytes=64)
        codes0_i = codes0[:].bitcast(I32)
        scales0_i = scales0[:].bitcast(I32)
        codes1_i = codes1[:].bitcast(I32)
        scales1_i = scales1[:].bitcast(I32)
        pair_codes_i = pair_codes[:].bitcast(I32)
        pair_scales_i = pair_scales[:].bitcast(I32)
        late_codes_i = late_codes[:].bitcast(I32)
        late_scales_i = late_scales[:].bitcast(I32)

        nc.vector.memset(w_scales[:].rearrange("p g n -> p (g n)").bitcast(I32), 0)
        nc.gpsimd.memset(edge_sb[:, 0, :].bitcast(F32), 0.0)
        nc.gpsimd.memset(nodes2[ALL_NODES:P].rearrange("p c f -> p (c f)").bitcast(F32), 0.0)
        make_identity(nc, ident[:])
        nc.gpsimd.memset(scales0_i[:, 0:2, :], 0)
        nc.gpsimd.memset(scales1_i[:, 0, :], 0)
        nc.gpsimd.memset(pair_scales_i, 0)
        nc.gpsimd.memset(late_scales_i, 0)
        nc.gpsimd.memset(late_grouped[HALF:P, 0].rearrange("p r t -> p (r t)").bitcast(F32), 0.0)
        nc.gpsimd.memset(late_grouped[:, 3].rearrange("p r t -> p (r t)").bitcast(F32), 0.0)

        nc.scalar.dma_start(
            out=nodes2[0:ALL_NODES],
            in_=node_fts.flatten_outer_dims().unsqueeze(1).to_broadcast([ALL_NODES, 2, NODE_IN]),
        )
        edge_rows = edge_fts.flatten_outer_dims().rearrange("(j r) e -> r j e", r=P)

        def load_edges(lo, hi):
            nc.sync.dma_start(out=edge_sb[:, 1 + lo : 1 + hi, :], in_=edge_rows[:, lo:hi, :])

        node_words = nodes2[:].rearrange("p c f -> p (c f)").bitcast(F32)
        edge_words = edge_sb[:].rearrange("p j e -> p (j e)").bitcast(F32)

        def transposed(planes, words, first):
            for u in range(2):
                nc.tensor.transpose(planes[:, u, :], words[:, first + u : first + 2 * P : 2], ident[:])

        def two_planes(lo, bank_tile):
            return bank_tile[:, lo : lo + 2 * P].rearrange("p (u r) -> p u r", u=2)

        def regrouped(t):
            return t.rearrange("p r t -> p (r t)").bitcast(F32).rearrange("p (r u) -> p r u", u=2)

        def warm_tensor(count):
            unused = psum.tile([P, BANK], F32, tag="bank")
            for again in range(count):
                nc.tensor.matmul(
                    out=unused[:],
                    lhsT=nodes2[:, 0, 0:P],
                    rhs=edge_sb[:, 1:3, :].rearrange("p j e -> p (j e)"),
                    start=True,
                    stop=True,
                )

        def pair_planes(first, last):
            bank_tile = psum.tile([P, BANK], F32, tag="bank")
            planes = bank_tile[:, 0 : 2 * P * (last - first)].rearrange("p (q u r) -> p q u r", u=2, r=P)
            for q in range(first, last):
                transposed(planes[:, q - first], edge_words, P * (2 * q + 1))
            return planes

        def dst_of_pass1(grouped, b):
            nc.scalar.copy(
                out=grouped[0:HALF].rearrange("p r t -> p (r t)").bitcast(F32).rearrange(
                    "p (i k u) -> p i k u", i=I_PER_TILE, u=2
                ),
                in_=second_planes[0:HALF, :, NODES * b : NODES * (b + 1)]
                .rearrange("p u k -> p k u")
                .unsqueeze(1)
                .to_broadcast([HALF, I_PER_TILE, NODES, 2]),
            )

        def quantise(codes, scales, grouped):
            nc.vector.quantize_mx(
                out=codes.rearrange("p a c -> p (a c)").bitcast(FP8X4),
                scales=scales.rearrange("p a c -> p (a c)"),
                in_=grouped.rearrange("p a r t -> p (a r t)"),
            )

        def pair_quantise(first, last):
            quantise(pair_codes[:, first:last], pair_scales[:, first:last], pair_grouped[:, first:last])

        def pair_copy(first, last, planes):
            nc.scalar.copy(
                out=pair_grouped[:, first:last]
                .rearrange("p q r t -> p (q r t)")
                .bitcast(F32)
                .rearrange("p (q r u) -> p q r u", q=last - first, u=2),
                in_=planes.rearrange("p q u r -> p q r u"),
            )

        def dst_of_pass0(copy, grouped, b):
            copy(
                out=grouped.rearrange("p r t -> p (r t)").bitcast(F32).rearrange(
                    "p (i k u) -> p i k u", i=I_PER_TILE, u=2
                ),
                in_=first_planes[:, :, NODES * b : NODES * (b + 1)]
                .rearrange("p u k -> p k u")
                .unsqueeze(1)
                .to_broadcast([P, I_PER_TILE, NODES, 2]),
            )

        def spread_src(b, codes_i, scales_i):
            tiles = slice(1 + TILES_PER_GRAPH * b, 1 + TILES_PER_GRAPH * (b + 1))
            for out_i, source in ((codes0_i, codes_i[0:SRC_PARTS, 0:P:REP]), (scales0_i, scales_i[0:SRC_PARTS])):
                view = out_i[0:SRC_PARTS, tiles, :].rearrange("p j (i k) -> p (j i) k", i=I_PER_TILE)
                nc.vector.tensor_copy(out=view, in_=source.unsqueeze(2).to_broadcast(list(view.shape)))

        def repeat(copy, out_view, source):
            copy(out=out_view, in_=source.unsqueeze(1).to_broadcast(list(out_view.shape)))

        def edge_moves(first, last, second_tiles):
            for e, copy in enumerate((nc.sync.dma_start, second_tiles)):
                places = slice(place_of(first, e), place_of(last - 1, e) + 1)
                for out_i, in_i in ((codes1_i, pair_codes_i), (scales1_i, pair_scales_i)):
                    copy(out=out_i[HALF:P, places, :], in_=in_i[HALF * e : HALF * (e + 1), first:last, :])

        out_rows = out.flatten_outer_dims()

        def row_tile(j):
            result = results.tile([P, HID], F32)
            for c in range(COL_TILES):
                acc = psum.tile([P, BANK], F32, tag="bank")
                place = place_of(j // 2, j % 2)
                operands = (
                    (codes0[:, 1 + j, :], scales0[:, 1 + j, :]),
                    (codes1[:, place, :], scales1[:, place, :]),
                )
                for g in range(PASSES):
                    codes, scales = operands[g]
                    nc.tensor.matmul_mx(
                        out=acc[:],
                        lhsT=codes.bitcast(FP8X4),
                        lhsT_scale=scales,
                        rhs=w_words[:, g, 2 * BANK * c : 2 * BANK * (c + 1)].bitcast(FP4X4),
                        rhs_scale=w_scales[:, g, BANK * c : BANK * (c + 1)],
                        start=(g == 0),
                        stop=(g == PASSES - 1),
                    )
                tenth = tenths.tile([P, BANK], F32)
                nc.scalar.activation(out=tenth[:], in_=acc[:], func=COPY, scale=NEG_SLOPE)
                nc.vector.tensor_tensor(out=result[:, BANK * c : BANK * (c + 1)], in0=acc[:], in1=tenth[:], op=MAX)
                if j in (0, ROW_TILES - 1):
                    cols = slice(BANK * c, BANK * (c + 1))
                    nc.sync.dma_start(out=out_rows[P * j : P * (j + 1), cols], in_=result[:, cols])
            if 0 < j < ROW_TILES - 1:
                nc.sync.dma_start(out=out_rows[P * j : P * (j + 1), :], in_=result[:])

        def prepare_pairs(first, last):
            planes = [pair_planes(q, q + 2) for q in range(first, last, 2)]
            for q in range(first, last, 2):
                pair_copy(q, q + 2, planes[(q - first) // 2])
            pair_quantise(first, last)
            edge_moves(first, last, nc.gpsimd.tensor_copy)

        def src_copy(copy, grouped, b):
            copy(
                out=grouped.rearrange("p c t -> p (c t)").bitcast(F32).rearrange("p (n r u) -> p n r u", r=REP, u=2),
                in_=first_planes[:, :, NODES * b : NODES * (b + 1)]
                .rearrange("p u n -> p n u")
                .unsqueeze(2)
                .to_broadcast([P, NODES, REP, 2]),
            )

        def load_weights(h):
            cols = slice(HID * h, HID * (h + 1))
            nc.sync.dma_start(
                out=w_words[:, :, cols].bitcast(I32),
                in_=Wt_words[:, :, cols].rearrange("g p n -> p g n").bitcast(I32),
            )

        with tc.manual_schedule(
            engines={
                mybir.EngineType.PE,
                mybir.EngineType.Activation,
                mybir.EngineType.DVE,
                mybir.EngineType.SP,
                mybir.EngineType.Pool,
            }
        ):
            load_edges(0, 4)
            for q in range(4):
                nc.sync.dma_start(
                    out=w_scales[32 * q : 32 * q + 4].bitcast(I32),
                    in_=Wt_scales[:, 4 * q : 4 * q + 4, :].rearrange("g r n -> r g n").bitcast(I32),
                )
            load_weights(0)
            load_weights(1)
            load_edges(4, 8)

            first_t = psum.tile([P, BANK], F32, tag="bank")
            second_t = psum.tile([P, BANK], F32, tag="bank")
            first_planes = two_planes(0, first_t)
            second_planes = two_planes(0, second_t)
            transposed(first_planes, node_words, 0)
            transposed(second_planes, node_words, HALF)
            tile0_t = psum.tile([P, BANK], F32, tag="bank")
            tile0_planes = two_planes(0, tile0_t)
            transposed(tile0_planes, edge_words, 0)
            planes = pair_planes(0, 2)

            for j, upper in enumerate((tile0_planes, planes[:, 0])):
                dst_of_pass1(first_grouped[:, j], 0)
                nc.scalar.copy(
                    out=regrouped(first_grouped[HALF:P, j]), in_=upper[HALF:P].rearrange("p u r -> p r u")
                )
            pair_copy(1, 2, planes[:, 1:2])
            dst_of_pass1(late_grouped[:, 0], 1)

            src_copy(nc.vector.tensor_copy, head_grouped[:, 0], 0)
            dst_of_pass0(nc.vector.tensor_copy, head_grouped[:, 1], 0)
            src_copy(nc.scalar.copy, late_grouped[:, 1], 1)
            dst_of_pass0(nc.scalar.copy, late_grouped[:, 2], 1)
            quantise(codes0[:, 0:2], scales0[:, 0:2], head_grouped[:])
            quantise(codes1[:, 0:1], scales1[:, 0:1], first_grouped[:, 0:1])
            spread_src(0, codes0_i[:, 0, :], scales0_i[:, 0, :])
            nc.vector.tensor_copy(out=codes0_i[SRC_PARTS:P, 2, :], in_=codes0_i[SRC_PARTS:P, 1, :])
            repeat(nc.vector.tensor_copy, scales0_i[SRC_PARTS:P, 2:9, :], scales0_i[SRC_PARTS:P, 1, :])
            repeat(nc.vector.tensor_copy, scales1_i[0:HALF, 2:8, :], scales1_i[0:HALF, 0, :])
            quantise(codes1[:, 1:2], scales1[:, 1:2], first_grouped[:, 1:2])
            pair_quantise(1, 2)
            edge_moves(1, 2, nc.sync.dma_start)
            repeat(nc.sync.dma_start, codes1_i[0:HALF, 2:8, :], codes1_i[0:HALF, 0, :])
            repeat(nc.sync.dma_start, codes0_i[SRC_PARTS:P, 3:9, :], codes0_i[SRC_PARTS:P, 1, :])
            load_edges(8, 16)
            quantise(late_codes[:], late_scales[:], late_grouped[:])
            spread_src(1, late_codes_i[:, 1, :], late_scales_i[:, 1, :])
            warm_tensor(4)

            row_tile(0)
            prepare_pairs(2, 4)
            row_tile(1)
            row_tile(2)
            prepare_pairs(4, 8)
            for tile in (8, 12):
                for first, ops, parts, slot in (
                    (tile, (codes1_i, scales1_i), slice(0, HALF), 0),
                    (1 + tile, (codes0_i, scales0_i), slice(SRC_PARTS, P), 2),
                ):
                    for out_i, source in zip(ops, (late_codes_i, late_scales_i)):
                        repeat(nc.gpsimd.tensor_copy, out_i[parts, first : first + 4, :], source[parts, slot, :])
            for j in range(3, ROW_TILES):
                row_tile(j)
